import numpy as np
import ml_dtypes


def mxq(x, axis, fmt="e4m3"):
    dtype, down = {"e4m3": (ml_dtypes.float8_e4m3fn, 7), "e5m2": (ml_dtypes.float8_e5m2, 14)}[fmt]
    v = np.moveaxis(np.asarray(x, np.float32).astype(ml_dtypes.bfloat16).astype(np.float64), axis, -1)
    blocks = v.reshape(v.shape[:-1] + (-1, 32))
    amax = np.abs(blocks).max(-1, keepdims=True)
    byte = np.maximum(np.where(amax > 0, np.frexp(amax)[1] - 1 + 127, 0) - down, 1)
    scale = np.exp2(byte - 127.0)
    codes = (blocks / scale).astype(np.float32).astype(dtype).astype(np.float64)
    return np.moveaxis((codes * scale).reshape(v.shape), -1, axis)


WIDE = False


def mx_kscale(k):
    if not WIDE:
        return np.ones(k)
    levels = np.array([10, -10, 5, -5, 0])
    a = np.random.permutation(np.resize(levels, k // 512 * 4)).reshape(k // 512, 4)
    idx = np.arange(k)
    return np.exp2(a[idx // 512, idx % 128 // 32])


BF16 = ml_dtypes.bfloat16


def bf(x):
    return np.asarray(x, np.float32).astype(BF16)


def f64(x):
    return np.asarray(x).astype(np.float64)


B, O, A, H, Z = 256, 512, 512, 1536, 512
I = O + Z + A


def sigmoid(v):
    return 1.0 / (1.0 + np.exp(-v))


def setup_inputs():
    s = mx_kscale(I)
    return {
        "x_t": bf(np.random.standard_normal((B, O)) * s[:O]),
        "z_t": bf(np.random.standard_normal((B, Z)) * 1.4 * s[O:O + Z]),
        "a_prev": bf(np.random.standard_normal((B, A)) * s[O + Z:]),
        "h_prev": bf(np.random.standard_normal((B, H))),
        "w_ih": bf(np.random.standard_normal((3 * H, I)) / np.sqrt(I) / s[None, :]),
        "w_hh": bf(np.random.standard_normal((3 * H, H)) / np.sqrt(H)),
        "b_ih": bf(np.random.standard_normal(3 * H) * 0.2),
        "b_hh": bf(np.random.standard_normal(3 * H) * 0.2),
    }


def reference(x_t, z_t, a_prev, h_prev, w_ih, w_hh, b_ih, b_hh):
    h = f64(h_prev)
    rnn_in = np.concatenate([f64(x_t), f64(z_t), f64(a_prev)], -1)
    gi = (mxq(rnn_in, 1, "e4m3") @ mxq(f64(w_ih), 1, "e4m3").T) + f64(b_ih)
    gh = (mxq(h, 1, "e4m3") @ mxq(f64(w_hh), 1, "e4m3").T) + f64(b_hh)
    i_r, i_z, i_n = gi[:, :H], gi[:, H:2 * H], gi[:, 2 * H:]
    h_r, h_z, h_n = gh[:, :H], gh[:, H:2 * H], gh[:, 2 * H:]
    r = sigmoid(i_r + h_r)
    zg = sigmoid(i_z + h_z)
    n = np.tanh(i_n + r * h_n)
    return (1.0 - zg) * n + zg * h

@@ -1,0 +1,320 @@
+from contextlib import ExitStack
+
+import concourse.mybir as mybir
+from concourse.masks import make_identity
+
+F32 = mybir.dt.float32
+BF16 = mybir.dt.bfloat16
+U32 = mybir.dt.uint32
+U8 = mybir.dt.uint8
+FP8X4 = mybir.dt.float8_e4m3fn_x4
+ACT = mybir.ActivationFunctionType
+ALU = mybir.AluOpType
+
+P = 128
+BATCH = 256
+HALVES = BATCH // P
+K = 1536
+HID = 1536
+K_PASS = 4 * P
+PASSES = K // K_PASS
+SLAB_WORDS = K_PASS // 2
+CHUNK = 2 * P
+CHUNKS = HID // CHUNK
+TILE_SLABS = 2 * PASSES
+UNIT_SLABS = 2 * TILE_SLABS
+QUAD = 4
+UNIT_QUADS = UNIT_SLABS // QUAD
+BANK_SLABS = 2
+UNIT_BANKS = UNIT_SLABS // BANK_SLABS
+
+GATES = ("r", "n", "z")
+GATE_BLOCK = {"r": 0, "z": 1, "n": 2}
+UNITS = CHUNKS * len(GATES)
+
+LOAD_AHEAD = 3
+TRANSPOSE_BANKS = 5
+SUM_BANKS = 3
+VECTOR_BANK = 2
+
+FLOPS = 2 * 2 * BATCH * K * 3 * HID
+
+
+def tile_vrnncell_pc_kernel(tc, x_t, z_t, a_prev, h_prev, w_ih, w_hh, b_ih, b_hh, out):
+    nc = tc.nc
+    with ExitStack() as ctx:
+        const = ctx.enter_context(tc.tile_pool(name="const", bufs=1))
+        wpool = ctx.enter_context(tc.tile_pool(name="weights", bufs=2 * (LOAD_AHEAD + 1)))
+        gpool = ctx.enter_context(tc.tile_pool(name="grouped", bufs=2 * UNIT_QUADS))
+        qpool = ctx.enter_context(tc.tile_pool(name="quantised", bufs=3 * UNIT_QUADS))
+        epool = ctx.enter_context(tc.tile_pool(name="gates", bufs=2))
+        tpsum = ctx.enter_context(tc.psum_pool(name="transposed", bufs=TRANSPOSE_BANKS))
+        spsum = ctx.enter_context(tc.psum_pool(name="sums", bufs=SUM_BANKS))
+        ctx.enter_context(tc.manual_schedule())
+
+        ident = const.tile([P, P], F32)
+        make_identity(nc, ident[:])
+
+        warm = const.tile([P, 1], F32)
+        nc.vector.memset(warm[:], 0.0)
+        nc.scalar.activation(out=warm[:], in_=warm[:], func=ACT.Sigmoid)
+
+        def transpose_slabs(slabs):
+            bank = tpsum.tile([P, BANK_SLABS, 2, P], F32, tag="bank")
+            for j, words in enumerate(slabs):
+                for u in range(2):
+                    nc.tensor.transpose(bank[:, j, u, :], words[:, u * P : (u + 1) * P], ident[:])
+            return bank
+
+        def copy_grouped(engine_copy, grouped_words, bank):
+            engine_copy(
+                out=grouped_words.rearrange("p (s r u) -> p s r u", s=BANK_SLABS, u=2),
+                in_=bank[:].rearrange("p s u r -> p s r u"),
+            )
+
+        weight_words = {}
+        grouped_of = {}
+        codes_of = {}
+
+        def load_unit(i):
+            chunk, g = divmod(i, len(GATES))
+            row0 = GATE_BLOCK[GATES[g]] * HID + chunk * CHUNK
+            views = []
+            for w in (w_ih, w_hh):
+                wt = wpool.tile([P, 2 * K], BF16, tag="w")
+                nc.sync.dma_start(out=wt[:], in_=w[row0 : row0 + CHUNK, :].rearrange("(p e) k -> p (e k)", e=2))
+                views.append(wt[:].bitcast(F32))
+            weight_words[i] = views
+
+        def slab_words(i, s):
+            tile_words = weight_words[i][s // TILE_SLABS]
+            first = (s % TILE_SLABS) * SLAB_WORDS
+            return tile_words[:, first : first + SLAB_WORDS]
+
+        def transpose_unit(i):
+            tiles = []
+            for q in range(UNIT_QUADS):
+                grouped = gpool.tile([P, QUAD * K_PASS], BF16, tag="grouped", align_bytes=64)
+                words = grouped[:].bitcast(F32)
+                for half in range(QUAD // BANK_SLABS):
+                    s = q * QUAD + half * BANK_SLABS
+                    bank = transpose_slabs([slab_words(i, s), slab_words(i, s + 1)])
+                    by_vector = s // BANK_SLABS == VECTOR_BANK
+                    copy_grouped(
+                        nc.vector.tensor_copy if by_vector else nc.scalar.copy,
+                        words[:, half * BANK_SLABS * SLAB_WORDS : (half + 1) * BANK_SLABS * SLAB_WORDS],
+                        bank,
+                    )
+                tiles.append(grouped)
+            grouped_of[i] = tiles
+
+        def quantise_unit(i):
+            pairs = []
+            for grouped in grouped_of[i]:
+                codes = qpool.tile([P, QUAD * P], U32, tag="codes", align_bytes=64)
+                scales = qpool.tile([P, QUAD * P], U8, tag="scales", align_bytes=64)
+                nc.vector.quantize_mx(out=codes[:].bitcast(FP8X4), scales=scales[:], in_=grouped[:])
+                pairs.append((codes, scales))
+            codes_of[i] = pairs
+
+        act_codes = []
+        act_scales = []
+        act_grouped = []
+
+        def load_activations():
+            raw = []
+            for name, src in (("x", x_t), ("z", z_t), ("a", a_prev), ("h", h_prev)):
+                width = src.shape[1]
+                t = const.tile([P, HALVES * width], BF16, name="raw_" + name)
+                nc.sync.dma_start(out=t[:], in_=src.rearrange("(p h) k -> p (h k)", h=HALVES))
+                raw.append(t[:].bitcast(F32).rearrange("p (h w) -> p h w", h=HALVES))
+            return raw
+
+        def prepare_activations(raw):
+            x_w, z_w, a_w, h_w = raw
+            pass_words = [
+                [x_w, z_w, a_w],
+                [h_w[:, :, g * SLAB_WORDS : (g + 1) * SLAB_WORDS] for g in range(PASSES)],
+            ]
+            for m in range(2):
+                grouped = const.tile([P, PASSES * HALVES * K_PASS], BF16, name="act_grouped%d" % m, align_bytes=64)
+                words = grouped[:].bitcast(F32)
+                for g in range(PASSES):
+                    bank = transpose_slabs([pass_words[m][g][:, h, :] for h in range(HALVES)])
+                    copy_grouped(
+                        nc.scalar.copy if (m * PASSES + g) % 2 == 0 else nc.vector.tensor_copy,
+                        words[:, g * HALVES * SLAB_WORDS : (g + 1) * HALVES * SLAB_WORDS],
+                        bank,
+                    )
+                act_grouped.append(grouped)
+            for m in range(2):
+                codes = const.tile([P, PASSES, BATCH], U32, name="act_codes%d" % m, align_bytes=64)
+                scales = const.tile([P, PASSES, BATCH], U8, name="act_scales%d" % m, align_bytes=64)
+                for g in range(PASSES):
+                    nc.vector.quantize_mx(
+                        out=codes[:, g, :].bitcast(FP8X4),
+                        scales=scales[:, g, :],
+                        in_=act_grouped[m][:, g * HALVES * K_PASS : (g + 1) * HALVES * K_PASS],
+                    )
+                act_codes.append(codes)
+                act_scales.append(scales)
+
+        B_HH_ROW = 32
+        BIAS_ROWS = 3 * CHUNKS
+
+        def load_biases():
+            bias_rows = const.tile([P, CHUNK], BF16)
+            nc.vector.memset(bias_rows[:], 0.0)
+            nc.sync.dma_start(out=bias_rows[0:BIAS_ROWS, :], in_=b_ih.rearrange("(j w) -> j w", w=CHUNK))
+            nc.sync.dma_start(
+                out=bias_rows[B_HH_ROW : B_HH_ROW + BIAS_ROWS, :], in_=b_hh.rearrange("(j w) -> j w", w=CHUNK)
+            )
+            return bias_rows
+
+        def prepare_biases(bias_rows):
+            bank = tpsum.tile([P, BANK_SLABS, 2, P], F32, tag="bank")
+            nc.tensor.transpose(bank[:, 0, 0, :], bias_rows[:].bitcast(F32), ident[:])
+            bias = const.tile([P, P, 2], F32)
+            nc.vector.tensor_copy(
+                out=bias[:].rearrange("p j e -> p (j e)"), in_=bank[:, 0, 0, :].bitcast(BF16)
+            )
+            both = const.tile([P, BIAS_ROWS, 2], F32)
+            nc.vector.tensor_tensor(
+                out=both[:], in0=bias[:, 0:BIAS_ROWS, :], in1=bias[:, B_HH_ROW : B_HH_ROW + BIAS_ROWS, :], op=ALU.add
+            )
+            return bias, both
+
+        sums_of = {}
+
+        def multiply_unit(i):
+            apart = GATES[i % len(GATES)] == "n"
+            banks = [spsum.tile([P, 2, BATCH], F32, tag="sums", name="sums%d" % b) for b in range(2 if apart else 1)]
+            pairs = codes_of[i]
+            for e in range(2):
+                for m in range(2):
+                    for g in range(PASSES):
+                        s = (m * 2 + e) * PASSES + g
+                        codes, scales = pairs[s // QUAD]
+                        cols = slice((s % QUAD) * P, (s % QUAD + 1) * P)
+                        nc.tensor.matmul_mx(
+                            out=banks[m if apart else 0][:, e, :],
+                            lhsT=codes[:, cols].bitcast(FP8X4),
+                            lhsT_scale=scales[:, cols],
+                            rhs=act_codes[m][:, g, :].bitcast(FP8X4),
+                            rhs_scale=act_scales[m][:, g, :],
+                            start=(g == 0 and (apart or m == 0)),
+                            stop=(g == PASSES - 1 and (apart or m == 1)),
+                        )
+            sums_of[i] = banks
+
+        gate_tiles = {}
+
+        def column(table, block, chunk, e):
+            return table[:, GATE_BLOCK[block] * CHUNKS + chunk, e : e + 1]
+
+        def sigmoid_gate(i, name):
+            chunk = i // len(GATES)
+            (bank,) = sums_of[i]
+            gate = epool.tile([P, 2, BATCH], F32, tag=name, name="gate_" + name)
+            for e in range(2):
+                nc.scalar.activation(
+                    out=gate[:, e, :], in_=bank[:, e, :], func=ACT.Sigmoid, bias=column(both, name, chunk, e)
+                )
+            gate_tiles[(chunk, name)] = gate
+
+        def candidate_input(i):
+            chunk = i // len(GATES)
+            bank_i, bank_h = sums_of[i]
+            r = gate_tiles[(chunk, "r")]
+            pre = epool.tile([P, 2, BATCH], F32, tag="pre")
+            for e in range(2):
+                nc.vector.scalar_tensor_tensor(
+                    out=pre[:, e, :],
+                    in0=bank_h[:, e, :],
+                    scalar=bias[:, B_HH_ROW + GATE_BLOCK["n"] * CHUNKS + chunk, e : e + 1],
+                    in1=r[:, e, :],
+                    op0=ALU.add,
+                    op1=ALU.mult,
+                )
+            nc.vector.tensor_tensor(out=pre[:], in0=pre[:], in1=bank_i[:], op=ALU.add)
+            gate_tiles[(chunk, "pre")] = pre
+
+        def candidate(chunk):
+            pre = gate_tiles[(chunk, "pre")]
+            n = epool.tile([P, 2, BATCH], F32, tag="n")
+            for e in range(2):
+                nc.scalar.activation(out=n[:, e, :], in_=pre[:, e, :], func=ACT.Tanh, bias=column(bias, "n", chunk, e))
+            g, u = divmod(chunk, 2)
+            h_t = act_grouped[1][:].rearrange("p (g b t) -> p g b t", g=PASSES, t=4)
+            diff = epool.tile([P, 2, BATCH], F32, tag="diff")
+            nc.vector.tensor_tensor(
+                out=diff[:], in0=h_t[:, g, :, 2 * u : 2 * u + 2].rearrange("p b e -> p e b"), in1=n[:], op=ALU.subtract
+            )
+            gate_tiles[(chunk, "n")] = n
+            gate_tiles[(chunk, "diff")] = diff
+
+        def blend(chunk):
+            zg = gate_tiles[(chunk, "z")]
+            diff = gate_tiles[(chunk, "diff")]
+            n = gate_tiles[(chunk, "n")]
+            new = epool.tile([P, 2, BATCH], F32, tag="new")
+            nc.vector.tensor_tensor(out=diff[:], in0=zg[:], in1=diff[:], op=ALU.mult)
+            nc.vector.tensor_tensor(out=new[:], in0=diff[:], in1=n[:], op=ALU.add)
+            gate_tiles[(chunk, "new")] = new
+
+        def transpose_back(chunk):
+            new = gate_tiles[(chunk, "new")]
+            bank = tpsum.tile([P, HALVES, 2, P], F32, tag="bank")
+            for h in range(HALVES):
+                for e in range(2):
+                    nc.tensor.transpose(bank[:, h, e, :], new[:, e, h * P : (h + 1) * P], ident[:])
+            return bank
+
+        def store_chunk(chunk, bank):
+            rows = epool.tile([P, HALVES, CHUNK], F32, tag="rows")
+            nc.scalar.copy(
+                out=rows[:].rearrange("p h (q e) -> p h q e", e=2), in_=bank[:].rearrange("p h e q -> p h q e")
+            )
+            nc.scalar.dma_start(
+                out=out.rearrange("(p h) f -> p h f", h=HALVES)[:, :, chunk * CHUNK : (chunk + 1) * CHUNK],
+                in_=rows[:],
+            )
+
+        load_unit(0)
+        raw = load_activations()
+        bias_rows = load_biases()
+        for i in range(1, LOAD_AHEAD):
+            load_unit(i)
+
+        bias = None
+        both = None
+        for step in range(UNITS + 3):
+            if step + LOAD_AHEAD < UNITS:
+                load_unit(step + LOAD_AHEAD)
+
+            blended = step - 3
+            if 0 <= blended < UNITS and GATES[blended % len(GATES)] == "z":
+                store_chunk(blended // len(GATES), transpose_back(blended // len(GATES)))
+
+            if step < UNITS:
+                transpose_unit(step)
+                quantise_unit(step)
+            if step == 0:
+                prepare_activations(raw)
+                bias, both = prepare_biases(bias_rows)
+
+            multiplied = step - 1
+            if 0 <= multiplied < UNITS:
+                multiply_unit(multiplied)
+
+            earlier = step - 2
+            if 0 <= earlier < UNITS and GATES[earlier % len(GATES)] == "n":
+                candidate(earlier // len(GATES))
+            if 0 <= multiplied < UNITS:
+                gate = GATES[multiplied % len(GATES)]
+                if gate == "n":
+                    candidate_input(multiplied)
+                else:
+                    sigmoid_gate(multiplied, gate)
+                if gate == "z":
+                    blend(multiplied // len(GATES))

@@ -35,7 +35,8 @@ UNITS = CHUNKS * len(GATES)
 LOAD_AHEAD = 3
 TRANSPOSE_BANKS = 5
 SUM_BANKS = 3
-VECTOR_BANK = 2
+TILE_BANKS = TILE_SLABS // BANK_SLABS
+VECTOR_BANK = 1
 
 FLOPS = 2 * 2 * BATCH * K * 3 * HID
 
@@ -99,7 +100,7 @@ def tile_vrnncell_pc_kernel(tc, x_t, z_t, a_prev, h_prev, w_ih, w_hh, b_ih, b_hh
                 for half in range(QUAD // BANK_SLABS):
                     s = q * QUAD + half * BANK_SLABS
                     bank = transpose_slabs([slab_words(i, s), slab_words(i, s + 1)])
-                    by_vector = s // BANK_SLABS == VECTOR_BANK
+                    by_vector = (s // BANK_SLABS) % TILE_BANKS == VECTOR_BANK
                     copy_grouped(
                         nc.vector.tensor_copy if by_vector else nc.scalar.copy,
                         words[:, half * BANK_SLABS * SLAB_WORDS : (half + 1) * BANK_SLABS * SLAB_WORDS],

@@ -35,8 +35,12 @@ UNITS = CHUNKS * len(GATES)
 LOAD_AHEAD = 3
 TRANSPOSE_BANKS = 5
 SUM_BANKS = 3
-TILE_BANKS = TILE_SLABS // BANK_SLABS
-VECTOR_BANK = 1
+VECTOR_BANK = 2
+
+MULTIPLY_AFTER = 1
+TANH_AFTER = 2
+BLEND_AFTER = 2
+STORE_AFTER = 6
 
 FLOPS = 2 * 2 * BATCH * K * 3 * HID
 
@@ -92,7 +96,7 @@ def tile_vrnncell_pc_kernel(tc, x_t, z_t, a_prev, h_prev, w_ih, w_hh, b_ih, b_hh
             first = (s % TILE_SLABS) * SLAB_WORDS
             return tile_words[:, first : first + SLAB_WORDS]
 
-        def transpose_unit(i):
+        def transpose_unit(i, vector_share):
             tiles = []
             for q in range(UNIT_QUADS):
                 grouped = gpool.tile([P, QUAD * K_PASS], BF16, tag="grouped", align_bytes=64)
@@ -100,7 +104,7 @@ def tile_vrnncell_pc_kernel(tc, x_t, z_t, a_prev, h_prev, w_ih, w_hh, b_ih, b_hh
                 for half in range(QUAD // BANK_SLABS):
                     s = q * QUAD + half * BANK_SLABS
                     bank = transpose_slabs([slab_words(i, s), slab_words(i, s + 1)])
-                    by_vector = (s // BANK_SLABS) % TILE_BANKS == VECTOR_BANK
+                    by_vector = (s // BANK_SLABS) % (UNIT_BANKS // vector_share) == VECTOR_BANK
                     copy_grouped(
                         nc.vector.tensor_copy if by_vector else nc.scalar.copy,
                         words[:, half * BANK_SLABS * SLAB_WORDS : (half + 1) * BANK_SLABS * SLAB_WORDS],
@@ -276,7 +280,7 @@ def tile_vrnncell_pc_kernel(tc, x_t, z_t, a_prev, h_prev, w_ih, w_hh, b_ih, b_hh
             nc.scalar.copy(
                 out=rows[:].rearrange("p h (q e) -> p h q e", e=2), in_=bank[:].rearrange("p h e q -> p h q e")
             )
-            nc.scalar.dma_start(
+            nc.sync.dma_start(
                 out=out.rearrange("(p h) f -> p h f", h=HALVES)[:, :, chunk * CHUNK : (chunk + 1) * CHUNK],
                 in_=rows[:],
             )
@@ -287,35 +291,35 @@ def tile_vrnncell_pc_kernel(tc, x_t, z_t, a_prev, h_prev, w_ih, w_hh, b_ih, b_hh
         for i in range(1, LOAD_AHEAD):
             load_unit(i)
 
+        def gate_of(i):
+            return GATES[i % len(GATES)] if 0 <= i < UNITS else None
+
         bias = None
         both = None
-        for step in range(UNITS + 3):
+        for step in range(UNITS + STORE_AFTER):
             if step + LOAD_AHEAD < UNITS:
                 load_unit(step + LOAD_AHEAD)
 
-            blended = step - 3
-            if 0 <= blended < UNITS and GATES[blended % len(GATES)] == "z":
-                store_chunk(blended // len(GATES), transpose_back(blended // len(GATES)))
+            if gate_of(step - STORE_AFTER) == "z":
+                chunk = (step - STORE_AFTER) // len(GATES)
+                store_chunk(chunk, transpose_back(chunk))
 
+            multiplied = step - MULTIPLY_AFTER
             if step < UNITS:
-                transpose_unit(step)
+                transpose_unit(step, vector_share=2 if gate_of(multiplied) == "z" else 1)
+            if gate_of(step - BLEND_AFTER) == "z":
+                blend((step - BLEND_AFTER) // len(GATES))
+            if step < UNITS:
                 quantise_unit(step)
             if step == 0:
                 prepare_activations(raw)
                 bias, both = prepare_biases(bias_rows)
 
-            multiplied = step - 1
-            if 0 <= multiplied < UNITS:
+            if gate_of(multiplied) is not None:
                 multiply_unit(multiplied)
-
-            earlier = step - 2
-            if 0 <= earlier < UNITS and GATES[earlier % len(GATES)] == "n":
-                candidate(earlier // len(GATES))
-            if 0 <= multiplied < UNITS:
-                gate = GATES[multiplied % len(GATES)]
-                if gate == "n":
-                    candidate_input(multiplied)
-                else:
-                    sigmoid_gate(multiplied, gate)
-                if gate == "z":
-                    blend(multiplied // len(GATES))
+            if gate_of(step - TANH_AFTER) == "n":
+                candidate((step - TANH_AFTER) // len(GATES))
+            if gate_of(multiplied) == "n":
+                candidate_input(multiplied)
+            elif gate_of(multiplied) is not None:
+                sigmoid_gate(multiplied, gate_of(multiplied))

@@ -40,7 +40,7 @@ VECTOR_BANK = 2
 MULTIPLY_AFTER = 1
 TANH_AFTER = 2
 BLEND_AFTER = 2
-STORE_AFTER = 6
+STORE_AFTER = 3
 
 FLOPS = 2 * 2 * BATCH * K * 3 * HID
 
@@ -258,12 +258,15 @@ def tile_vrnncell_pc_kernel(tc, x_t, z_t, a_prev, h_prev, w_ih, w_hh, b_ih, b_hh
             gate_tiles[(chunk, "n")] = n
             gate_tiles[(chunk, "diff")] = diff
 
-        def blend(chunk):
+        def blend_product(chunk):
             zg = gate_tiles[(chunk, "z")]
+            diff = gate_tiles[(chunk, "diff")]
+            nc.vector.tensor_tensor(out=diff[:], in0=zg[:], in1=diff[:], op=ALU.mult)
+
+        def blend_sum(chunk):
             diff = gate_tiles[(chunk, "diff")]
             n = gate_tiles[(chunk, "n")]
             new = epool.tile([P, 2, BATCH], F32, tag="new")
-            nc.vector.tensor_tensor(out=diff[:], in0=zg[:], in1=diff[:], op=ALU.mult)
             nc.vector.tensor_tensor(out=new[:], in0=diff[:], in1=n[:], op=ALU.add)
             gate_tiles[(chunk, "new")] = new
 
@@ -300,15 +303,16 @@ def tile_vrnncell_pc_kernel(tc, x_t, z_t, a_prev, h_prev, w_ih, w_hh, b_ih, b_hh
             if step + LOAD_AHEAD < UNITS:
                 load_unit(step + LOAD_AHEAD)
 
+            multiplied = step - MULTIPLY_AFTER
+            if gate_of(step - BLEND_AFTER) == "z":
+                blend_product((step - BLEND_AFTER) // len(GATES))
+            if step < UNITS:
+                transpose_unit(step, vector_share=2 if gate_of(multiplied) == "z" else 1)
             if gate_of(step - STORE_AFTER) == "z":
                 chunk = (step - STORE_AFTER) // len(GATES)
                 store_chunk(chunk, transpose_back(chunk))
-
-            multiplied = step - MULTIPLY_AFTER
-            if step < UNITS:
-                transpose_unit(step, vector_share=2 if gate_of(multiplied) == "z" else 1)
             if gate_of(step - BLEND_AFTER) == "z":
-                blend((step - BLEND_AFTER) // len(GATES))
+                blend_sum((step - BLEND_AFTER) // len(GATES))
             if step < UNITS:
                 quantise_unit(step)
             if step == 0:

@@ -21,26 +21,23 @@ PASSES = K // K_PASS
 SLAB_WORDS = K_PASS // 2
 CHUNK = 2 * P
 CHUNKS = HID // CHUNK
-TILE_SLABS = 2 * PASSES
-UNIT_SLABS = 2 * TILE_SLABS
-QUAD = 4
-UNIT_QUADS = UNIT_SLABS // QUAD
 BANK_SLABS = 2
-UNIT_BANKS = UNIT_SLABS // BANK_SLABS
+STEP_SLABS = 2 * PASSES
+STEP_BANKS = STEP_SLABS // BANK_SLABS
+WIDE_SLABS = 4
 
 GATES = ("r", "n", "z")
 GATE_BLOCK = {"r": 0, "z": 1, "n": 2}
 UNITS = CHUNKS * len(GATES)
+STEPS = 2 * UNITS
+CHUNK_STEPS = 2 * len(GATES)
 
-LOAD_AHEAD = 3
+LOAD_AHEAD = 4
 TRANSPOSE_BANKS = 5
 SUM_BANKS = 3
-VECTOR_BANK = 2
 
-MULTIPLY_AFTER = 1
-TANH_AFTER = 2
-BLEND_AFTER = 2
-STORE_AFTER = 3
+WHOLE_UNITS = 2
+RUN = 1
 
 FLOPS = 2 * 2 * BATCH * K * 3 * HID
 
@@ -50,9 +47,9 @@ def tile_vrnncell_pc_kernel(tc, x_t, z_t, a_prev, h_prev, w_ih, w_hh, b_ih, b_hh
     with ExitStack() as ctx:
         const = ctx.enter_context(tc.tile_pool(name="const", bufs=1))
         wpool = ctx.enter_context(tc.tile_pool(name="weights", bufs=2 * (LOAD_AHEAD + 1)))
-        gpool = ctx.enter_context(tc.tile_pool(name="grouped", bufs=2 * UNIT_QUADS))
-        qpool = ctx.enter_context(tc.tile_pool(name="quantised", bufs=3 * UNIT_QUADS))
-        epool = ctx.enter_context(tc.tile_pool(name="gates", bufs=2))
+        gpool = ctx.enter_context(tc.tile_pool(name="grouped", bufs=3))
+        qpool = ctx.enter_context(tc.tile_pool(name="quantised", bufs=4))
+        epool = ctx.enter_context(tc.tile_pool(name="gates", bufs=4))
         tpsum = ctx.enter_context(tc.psum_pool(name="transposed", bufs=TRANSPOSE_BANKS))
         spsum = ctx.enter_context(tc.psum_pool(name="sums", bufs=SUM_BANKS))
         ctx.enter_context(tc.manual_schedule())
@@ -81,88 +78,85 @@ def tile_vrnncell_pc_kernel(tc, x_t, z_t, a_prev, h_prev, w_ih, w_hh, b_ih, b_hh
         grouped_of = {}
         codes_of = {}
 
-        def load_unit(i):
+        def load_tile(i, m):
             chunk, g = divmod(i, len(GATES))
             row0 = GATE_BLOCK[GATES[g]] * HID + chunk * CHUNK
-            views = []
-            for w in (w_ih, w_hh):
-                wt = wpool.tile([P, 2 * K], BF16, tag="w")
-                nc.sync.dma_start(out=wt[:], in_=w[row0 : row0 + CHUNK, :].rearrange("(p e) k -> p (e k)", e=2))
-                views.append(wt[:].bitcast(F32))
-            weight_words[i] = views
+            wt = wpool.tile([P, 2 * K], BF16, tag="w")
+            w = (w_ih, w_hh)[m]
+            nc.sync.dma_start(out=wt[:], in_=w[row0 : row0 + CHUNK, :].rearrange("(p e) k -> p (e k)", e=2))
+            weight_words[(i, m)] = wt[:].bitcast(F32)
 
-        def slab_words(i, s):
-            tile_words = weight_words[i][s // TILE_SLABS]
-            first = (s % TILE_SLABS) * SLAB_WORDS
-            return tile_words[:, first : first + SLAB_WORDS]
+        def load_unit(i):
+            load_tile(i, 0)
+            load_tile(i, 1)
 
-        def transpose_unit(i, vector_share):
-            tiles = []
-            for q in range(UNIT_QUADS):
-                grouped = gpool.tile([P, QUAD * K_PASS], BF16, tag="grouped", align_bytes=64)
-                words = grouped[:].bitcast(F32)
-                for half in range(QUAD // BANK_SLABS):
-                    s = q * QUAD + half * BANK_SLABS
-                    bank = transpose_slabs([slab_words(i, s), slab_words(i, s + 1)])
-                    by_vector = (s // BANK_SLABS) % (UNIT_BANKS // vector_share) == VECTOR_BANK
-                    copy_grouped(
-                        nc.vector.tensor_copy if by_vector else nc.scalar.copy,
-                        words[:, half * BANK_SLABS * SLAB_WORDS : (half + 1) * BANK_SLABS * SLAB_WORDS],
-                        bank,
-                    )
-                tiles.append(grouped)
-            grouped_of[i] = tiles
+        def slab_words(step, s):
+            unit, half = divmod(step, 2)
+            j, g = divmod(s, PASSES)
+            m, e = (half, j) if unit < WHOLE_UNITS else (j, half)
+            first = (e * PASSES + g) * SLAB_WORDS
+            return weight_words[(unit, m)][:, first : first + SLAB_WORDS]
 
-        def quantise_unit(i):
-            pairs = []
-            for grouped in grouped_of[i]:
-                codes = qpool.tile([P, QUAD * P], U32, tag="codes", align_bytes=64)
-                scales = qpool.tile([P, QUAD * P], U8, tag="scales", align_bytes=64)
-                nc.vector.quantize_mx(out=codes[:].bitcast(FP8X4), scales=scales[:], in_=grouped[:])
-                pairs.append((codes, scales))
-            codes_of[i] = pairs
+        def transpose_step(step, vector_banks):
+            grouped = gpool.tile([P, STEP_SLABS * K_PASS], BF16, tag="grouped", align_bytes=64)
+            words = grouped[:].bitcast(F32)
+            bank_words = BANK_SLABS * SLAB_WORDS
+            for b in range(STEP_BANKS):
+                bank = transpose_slabs([slab_words(step, BANK_SLABS * b + j) for j in range(BANK_SLABS)])
+                copy_grouped(
+                    nc.vector.tensor_copy if b in vector_banks else nc.scalar.copy,
+                    words[:, b * bank_words : (b + 1) * bank_words],
+                    bank,
+                )
+            grouped_of[step] = grouped
+
+        def quantise(step, first, last):
+            if step not in codes_of:
+                codes = qpool.tile([P, STEP_SLABS * P], U32, tag="codes", align_bytes=64)
+                scales = qpool.tile([P, STEP_SLABS * P], U8, tag="scales", align_bytes=64)
+                codes_of[step] = (codes, scales)
+            codes, scales = codes_of[step]
+            cols = slice(first * P, last * P)
+            nc.vector.quantize_mx(
+                out=codes[:, cols].bitcast(FP8X4),
+                scales=scales[:, cols],
+                in_=grouped_of[step][:, first * K_PASS : last * K_PASS],
+            )
 
         act_codes = []
         act_scales = []
         act_grouped = []
 
-        def load_activations():
-            raw = []
-            for name, src in (("x", x_t), ("z", z_t), ("a", a_prev), ("h", h_prev)):
-                width = src.shape[1]
-                t = const.tile([P, HALVES * width], BF16, name="raw_" + name)
-                nc.sync.dma_start(out=t[:], in_=src.rearrange("(p h) k -> p (h k)", h=HALVES))
-                raw.append(t[:].bitcast(F32).rearrange("p (h w) -> p h w", h=HALVES))
-            return raw
+        def load_activation(name, src):
+            width = src.shape[1]
+            t = const.tile([P, HALVES * width], BF16, name="raw_" + name)
+            nc.sync.dma_start(out=t[:], in_=src.rearrange("(p h) k -> p (h k)", h=HALVES))
+            return t[:].bitcast(F32).rearrange("p (h w) -> p h w", h=HALVES)
 
-        def prepare_activations(raw):
-            x_w, z_w, a_w, h_w = raw
-            pass_words = [
-                [x_w, z_w, a_w],
-                [h_w[:, :, g * SLAB_WORDS : (g + 1) * SLAB_WORDS] for g in range(PASSES)],
-            ]
-            for m in range(2):
-                grouped = const.tile([P, PASSES * HALVES * K_PASS], BF16, name="act_grouped%d" % m, align_bytes=64)
-                words = grouped[:].bitcast(F32)
-                for g in range(PASSES):
-                    bank = transpose_slabs([pass_words[m][g][:, h, :] for h in range(HALVES)])
-                    copy_grouped(
-                        nc.scalar.copy if (m * PASSES + g) % 2 == 0 else nc.vector.tensor_copy,
-                        words[:, g * HALVES * SLAB_WORDS : (g + 1) * HALVES * SLAB_WORDS],
-                        bank,
-                    )
-                act_grouped.append(grouped)
-            for m in range(2):
-                codes = const.tile([P, PASSES, BATCH], U32, name="act_codes%d" % m, align_bytes=64)
-                scales = const.tile([P, PASSES, BATCH], U8, name="act_scales%d" % m, align_bytes=64)
-                for g in range(PASSES):
-                    nc.vector.quantize_mx(
-                        out=codes[:, g, :].bitcast(FP8X4),
-                        scales=scales[:, g, :],
-                        in_=act_grouped[m][:, g * HALVES * K_PASS : (g + 1) * HALVES * K_PASS],
-                    )
-                act_codes.append(codes)
-                act_scales.append(scales)
+        def prepare_activation(m, pass_words):
+            grouped = const.tile([P, PASSES * HALVES * K_PASS], BF16, name="act_grouped%d" % m, align_bytes=64)
+            words = grouped[:].bitcast(F32)
+            for g in range(PASSES):
+                bank = transpose_slabs([pass_words[g][:, h, :] for h in range(HALVES)])
+                copy_grouped(
+                    nc.scalar.copy if g % 2 == 1 else nc.vector.tensor_copy,
+                    words[:, g * HALVES * SLAB_WORDS : (g + 1) * HALVES * SLAB_WORDS],
+                    bank,
+                )
+            act_grouped.append(grouped)
+
+        def quantise_activation(m):
+            grouped = act_grouped[m]
+            codes = const.tile([P, PASSES, BATCH], U32, name="act_codes%d" % m, align_bytes=64)
+            scales = const.tile([P, PASSES, BATCH], U8, name="act_scales%d" % m, align_bytes=64)
+            for g in range(PASSES):
+                nc.vector.quantize_mx(
+                    out=codes[:, g, :].bitcast(FP8X4),
+                    scales=scales[:, g, :],
+                    in_=grouped[:, g * HALVES * K_PASS : (g + 1) * HALVES * K_PASS],
+                )
+            act_codes.append(codes)
+            act_scales.append(scales)
 
         B_HH_ROW = 32
         BIAS_ROWS = 3 * CHUNKS
@@ -170,8 +164,8 @@ def tile_vrnncell_pc_kernel(tc, x_t, z_t, a_prev, h_prev, w_ih, w_hh, b_ih, b_hh
         def load_biases():
             bias_rows = const.tile([P, CHUNK], BF16)
             nc.vector.memset(bias_rows[:], 0.0)
-            nc.sync.dma_start(out=bias_rows[0:BIAS_ROWS, :], in_=b_ih.rearrange("(j w) -> j w", w=CHUNK))
-            nc.sync.dma_start(
+            nc.scalar.dma_start(out=bias_rows[0:BIAS_ROWS, :], in_=b_ih.rearrange("(j w) -> j w", w=CHUNK))
+            nc.scalar.dma_start(
                 out=bias_rows[B_HH_ROW : B_HH_ROW + BIAS_ROWS, :], in_=b_hh.rearrange("(j w) -> j w", w=CHUNK)
             )
             return bias_rows
@@ -191,92 +185,122 @@ def tile_vrnncell_pc_kernel(tc, x_t, z_t, a_prev, h_prev, w_ih, w_hh, b_ih, b_hh
 
         sums_of = {}
 
-        def multiply_unit(i):
-            apart = GATES[i % len(GATES)] == "n"
-            banks = [spsum.tile([P, 2, BATCH], F32, tag="sums", name="sums%d" % b) for b in range(2 if apart else 1)]
-            pairs = codes_of[i]
-            for e in range(2):
-                for m in range(2):
+        def multiply(step, s, out_step, m, g, apart):
+            codes, scales = codes_of[step]
+            cols = slice(s * P, (s + 1) * P)
+            nc.tensor.matmul_mx(
+                out=sums_of[out_step][:, m if apart else 0, :],
+                lhsT=codes[:, cols].bitcast(FP8X4),
+                lhsT_scale=scales[:, cols],
+                rhs=act_codes[m][:, g, :].bitcast(FP8X4),
+                rhs_scale=act_scales[m][:, g, :],
+                start=(g == 0 and (apart or m == 0)),
+                stop=(g == PASSES - 1 and (apart or m == 1)),
+            )
+
+        def new_sums(step):
+            bank = spsum.tile([P, 2, BATCH], F32, tag="sums")
+            sums_of[step] = bank
+
+        def multiply_step(step):
+            unit, half = divmod(step, 2)
+            apart = GATES[unit % len(GATES)] == "n"
+            if unit < WHOLE_UNITS:
+                if half == 0:
+                    new_sums(2 * unit)
+                    new_sums(2 * unit + 1)
+                for e in range(2):
                     for g in range(PASSES):
-                        s = (m * 2 + e) * PASSES + g
-                        codes, scales = pairs[s // QUAD]
-                        cols = slice((s % QUAD) * P, (s % QUAD + 1) * P)
-                        nc.tensor.matmul_mx(
-                            out=banks[m if apart else 0][:, e, :],
-                            lhsT=codes[:, cols].bitcast(FP8X4),
-                            lhsT_scale=scales[:, cols],
-                            rhs=act_codes[m][:, g, :].bitcast(FP8X4),
-                            rhs_scale=act_scales[m][:, g, :],
-                            start=(g == 0 and (apart or m == 0)),
-                            stop=(g == PASSES - 1 and (apart or m == 1)),
-                        )
-            sums_of[i] = banks
+                        multiply(step, e * PASSES + g, 2 * unit + e, half, g, apart)
+                return
+            new_sums(step)
+            for m in range(2):
+                for g in range(PASSES):
+                    multiply(step, m * PASSES + g, step, m, g, apart)
 
         gate_tiles = {}
+
+        def gate_tile(chunk, e, name):
+            t = epool.tile([P, BATCH], F32, tag=name, name="gate_" + name)
+            gate_tiles[(chunk, e, name)] = t
+            return t
 
         def column(table, block, chunk, e):
             return table[:, GATE_BLOCK[block] * CHUNKS + chunk, e : e + 1]
 
-        def sigmoid_gate(i, name):
-            chunk = i // len(GATES)
-            (bank,) = sums_of[i]
-            gate = epool.tile([P, 2, BATCH], F32, tag=name, name="gate_" + name)
-            for e in range(2):
-                nc.scalar.activation(
-                    out=gate[:, e, :], in_=bank[:, e, :], func=ACT.Sigmoid, bias=column(both, name, chunk, e)
-                )
-            gate_tiles[(chunk, name)] = gate
+        def sigmoid_gate(chunk, e, name, step):
+            gate = gate_tile(chunk, e, name)
+            nc.scalar.activation(
+                out=gate[:], in_=sums_of[step][:, 0, :], func=ACT.Sigmoid, bias=column(both, name, chunk, e)
+            )
 
-        def candidate_input(i):
-            chunk = i // len(GATES)
-            bank_i, bank_h = sums_of[i]
-            r = gate_tiles[(chunk, "r")]
-            pre = epool.tile([P, 2, BATCH], F32, tag="pre")
-            for e in range(2):
-                nc.vector.scalar_tensor_tensor(
-                    out=pre[:, e, :],
-                    in0=bank_h[:, e, :],
-                    scalar=bias[:, B_HH_ROW + GATE_BLOCK["n"] * CHUNKS + chunk, e : e + 1],
-                    in1=r[:, e, :],
-                    op0=ALU.add,
-                    op1=ALU.mult,
-                )
-            nc.vector.tensor_tensor(out=pre[:], in0=pre[:], in1=bank_i[:], op=ALU.add)
-            gate_tiles[(chunk, "pre")] = pre
+        def candidate_product(chunk, e, step):
+            pre = gate_tile(chunk, e, "pre")
+            nc.vector.scalar_tensor_tensor(
+                out=pre[:],
+                in0=sums_of[step][:, 1, :],
+                scalar=bias[:, B_HH_ROW + GATE_BLOCK["n"] * CHUNKS + chunk, e : e + 1],
+                in1=gate_tiles[(chunk, e, "r")][:],
+                op0=ALU.add,
+                op1=ALU.mult,
+            )
 
-        def candidate(chunk):
-            pre = gate_tiles[(chunk, "pre")]
-            n = epool.tile([P, 2, BATCH], F32, tag="n")
-            for e in range(2):
-                nc.scalar.activation(out=n[:, e, :], in_=pre[:, e, :], func=ACT.Tanh, bias=column(bias, "n", chunk, e))
+        def candidate_sum(chunk, e, step):
+            pre = gate_tiles[(chunk, e, "pre")]
+            nc.vector.tensor_tensor(out=pre[:], in0=pre[:], in1=sums_of[step][:, 0, :], op=ALU.add)
+
+        def candidate_tanh(chunk, e):
+            n = gate_tile(chunk, e, "n")
+            nc.scalar.activation(
+                out=n[:], in_=gate_tiles[(chunk, e, "pre")][:], func=ACT.Tanh, bias=column(bias, "n", chunk, e)
+            )
+
+        def candidate_diff(chunk, e):
             g, u = divmod(chunk, 2)
             h_t = act_grouped[1][:].rearrange("p (g b t) -> p g b t", g=PASSES, t=4)
-            diff = epool.tile([P, 2, BATCH], F32, tag="diff")
+            diff = gate_tile(chunk, e, "diff")
             nc.vector.tensor_tensor(
-                out=diff[:], in0=h_t[:, g, :, 2 * u : 2 * u + 2].rearrange("p b e -> p e b"), in1=n[:], op=ALU.subtract
+                out=diff[:], in0=h_t[:, g, :, 2 * u + e], in1=gate_tiles[(chunk, e, "n")][:], op=ALU.subtract
             )
-            gate_tiles[(chunk, "n")] = n
-            gate_tiles[(chunk, "diff")] = diff
 
-        def blend_product(chunk):
-            zg = gate_tiles[(chunk, "z")]
-            diff = gate_tiles[(chunk, "diff")]
-            nc.vector.tensor_tensor(out=diff[:], in0=zg[:], in1=diff[:], op=ALU.mult)
+        def blend_product(chunk, e):
+            diff = gate_tiles[(chunk, e, "diff")]
+            nc.vector.tensor_tensor(out=diff[:], in0=gate_tiles[(chunk, e, "z")][:], in1=diff[:], op=ALU.mult)
 
-        def blend_sum(chunk):
-            diff = gate_tiles[(chunk, "diff")]
-            n = gate_tiles[(chunk, "n")]
-            new = epool.tile([P, 2, BATCH], F32, tag="new")
-            nc.vector.tensor_tensor(out=new[:], in0=diff[:], in1=n[:], op=ALU.add)
-            gate_tiles[(chunk, "new")] = new
+        def blend_sum(chunk, e):
+            new = gate_tile(chunk, e, "new")
+            nc.vector.tensor_tensor(
+                out=new[:], in0=gate_tiles[(chunk, e, "diff")][:], in1=gate_tiles[(chunk, e, "n")][:], op=ALU.add
+            )
 
         def transpose_back(chunk):
-            new = gate_tiles[(chunk, "new")]
             bank = tpsum.tile([P, HALVES, 2, P], F32, tag="bank")
             for h in range(HALVES):
                 for e in range(2):
-                    nc.tensor.transpose(bank[:, h, e, :], new[:, e, h * P : (h + 1) * P], ident[:])
+                    nc.tensor.transpose(
+                        bank[:, h, e, :], gate_tiles[(chunk, e, "new")][:, h * P : (h + 1) * P], ident[:]
+                    )
             return bank
+
+        def finish_last(chunk):
+            banks = []
+            for h in range(HALVES):
+                bank = tpsum.tile([P, HALVES, 2, P], F32, tag="bank")
+                banks.append(bank)
+            for e in range(2):
+                for h in range(HALVES):
+                    nc.tensor.transpose(
+                        banks[h][:, 0, e, :], gate_tiles[(chunk, e, "new")][:, h * P : (h + 1) * P], ident[:]
+                    )
+            for h, engine_copy in enumerate((nc.scalar.copy, nc.vector.tensor_copy)):
+                rows = epool.tile([P, CHUNK], F32, tag="last_rows")
+                engine_copy(
+                    out=rows[:].rearrange("p (q e) -> p q e", e=2), in_=banks[h][:, 0, :, :].rearrange("p e q -> p q e")
+                )
+                nc.sync.dma_start(
+                    out=out.rearrange("(p h) f -> p h f", h=HALVES)[:, h, chunk * CHUNK : (chunk + 1) * CHUNK],
+                    in_=rows[:],
+                )
 
         def store_chunk(chunk, bank):
             rows = epool.tile([P, HALVES, CHUNK], F32, tag="rows")
@@ -288,42 +312,86 @@ def tile_vrnncell_pc_kernel(tc, x_t, z_t, a_prev, h_prev, w_ih, w_hh, b_ih, b_hh
                 in_=rows[:],
             )
 
-        load_unit(0)
-        raw = load_activations()
+        def half_of(step):
+            chunk, rest = divmod(step, CHUNK_STEPS)
+            return (GATES[rest // 2] if 0 <= step < STEPS else None), chunk, rest % 2
+
+        x_w = load_activation("x", x_t)
+        z_w = load_activation("z", z_t)
+        a_w = load_activation("a", a_prev)
+        load_tile(0, 0)
+        h_w = load_activation("h", h_prev)
+        load_tile(0, 1)
         bias_rows = load_biases()
         for i in range(1, LOAD_AHEAD):
             load_unit(i)
 
-        def gate_of(i):
-            return GATES[i % len(GATES)] if 0 <= i < UNITS else None
+
+        multiplies = {0: [0], 2: [1], 3: [2], 5: [3]}
+        for s in range(4, STEPS):
+            at = s + 2
+            if RUN == 2 and at % 2 == 0:
+                at += 1
+            if at >= STEPS + 1:
+                at = STEPS + 1 if s == STEPS - 1 else STEPS
+            multiplies.setdefault(at, []).append(s)
+        sums_at = {0: 2, 1: 2, 2: 5, 3: 5}
+        for s, lst in multiplies.items():
+            for x in lst:
+                if x >= 4:
+                    sums_at[x] = s
+        sig = {}
+        for x in range(STEPS):
+            sig.setdefault(max(sums_at[x] + 1, max(sig, default=0) + 1), []).append(x)
+        sig_step = {x: s for s, lst in sig.items() for x in lst}
+        total = max(sig) + 3
+
+        def at(step, gate, delay):
+            return [half_of(x)[1:] + (x,) for x in range(STEPS) if sig_step[x] + delay == step and half_of(x)[0] == gate]
 
         bias = None
         both = None
-        for step in range(UNITS + STORE_AFTER):
-            if step + LOAD_AHEAD < UNITS:
-                load_unit(step + LOAD_AHEAD)
+        prepare_activation(0, [x_w, z_w, a_w])
+        quantise_activation(0)
+        for step in range(total):
+            if step % 2 == 0 and step // 2 + LOAD_AHEAD < UNITS:
+                load_unit(step // 2 + LOAD_AHEAD)
 
-            multiplied = step - MULTIPLY_AFTER
-            if gate_of(step - BLEND_AFTER) == "z":
-                blend_product((step - BLEND_AFTER) // len(GATES))
-            if step < UNITS:
-                transpose_unit(step, vector_share=2 if gate_of(multiplied) == "z" else 1)
-            if gate_of(step - STORE_AFTER) == "z":
-                chunk = (step - STORE_AFTER) // len(GATES)
-                store_chunk(chunk, transpose_back(chunk))
-            if gate_of(step - BLEND_AFTER) == "z":
-                blend_sum((step - BLEND_AFTER) // len(GATES))
-            if step < UNITS:
-                quantise_unit(step)
+            for c, e, x in at(step, "r", 0):
+                sigmoid_gate(c, e, "r", x)
+            for c, e, x in at(step, "z", 0):
+                sigmoid_gate(c, e, "z", x)
+            for c, e, x in at(step, "n", 0):
+                candidate_product(c, e, x)
+            for c, e, x in at(step, "n", 1):
+                candidate_tanh(c, e)
+            late = step > 3
+            if late and 1 <= step <= STEPS:
+                quantise(step - 1, 0, WIDE_SLABS)
+            for c, e, x in at(step, "n", 0):
+                candidate_sum(c, e, x)
+            for c, e, x in at(step, "z", 1):
+                blend_product(c, e)
+            if late and 1 <= step <= STEPS:
+                quantise(step - 1, WIDE_SLABS, STEP_SLABS)
+            if step < STEPS:
+                transpose_step(step, vector_banks=(0,) if step % 3 != 1 else ())
+            if step <= 3:
+                quantise(step, 0, WIDE_SLABS)
+                quantise(step, WIDE_SLABS, STEP_SLABS)
             if step == 0:
-                prepare_activations(raw)
+                prepare_activation(1, [h_w[:, :, g * SLAB_WORDS : (g + 1) * SLAB_WORDS] for g in range(PASSES)])
+                quantise_activation(1)
+            if step == 1:
                 bias, both = prepare_biases(bias_rows)
-
-            if gate_of(multiplied) is not None:
-                multiply_unit(multiplied)
-            if gate_of(step - TANH_AFTER) == "n":
-                candidate((step - TANH_AFTER) // len(GATES))
-            if gate_of(multiplied) == "n":
-                candidate_input(multiplied)
-            elif gate_of(multiplied) is not None:
-                sigmoid_gate(multiplied, gate_of(multiplied))
+            for c, e, x in at(step, "z", 2):
+                if e == 1 and c == CHUNKS - 1:
+                    finish_last(c)
+                elif e == 1:
+                    store_chunk(c, transpose_back(c))
+            for c, e, x in at(step, "z", 1):
+                blend_sum(c, e)
+            for c, e, x in at(step, "n", 2):
+                candidate_diff(c, e)
+            for x in multiplies.get(step, []):
+                multiply_step(x)

@@ -36,6 +36,7 @@ LOAD_AHEAD = 4
 TRANSPOSE_BANKS = 5
 SUM_BANKS = 3
 
+WARM = (6, 3, 2, 2, 2)
 WHOLE_UNITS = 2
 RUN = 1
 
@@ -60,6 +61,18 @@ def tile_vrnncell_pc_kernel(tc, x_t, z_t, a_prev, h_prev, w_ih, w_hh, b_ih, b_hh
         warm = const.tile([P, 1], F32)
         nc.vector.memset(warm[:], 0.0)
         nc.scalar.activation(out=warm[:], in_=warm[:], func=ACT.Sigmoid)
+
+        zeros = const.tile([P, 4 * P], BF16)
+        nc.vector.memset(zeros[:], 0.0)
+
+        def keep_warm(count):
+            if count == 0:
+                return
+            bank = spsum.tile([P, 2, BATCH], F32, tag="sums")
+            for i in range(count):
+                nc.tensor.matmul(
+                    bank[:].rearrange("p m b -> p (m b)"), lhsT=zeros[:, 0:P], rhs=zeros[:], start=True, stop=True
+                )
 
         def transpose_slabs(slabs):
             bank = tpsum.tile([P, BANK_SLABS, 2, P], F32, tag="bank")
@@ -335,10 +348,10 @@ def tile_vrnncell_pc_kernel(tc, x_t, z_t, a_prev, h_prev, w_ih, w_hh, b_ih, b_hh
             if at >= STEPS + 1:
                 at = STEPS + 1 if s == STEPS - 1 else STEPS
             multiplies.setdefault(at, []).append(s)
-        sums_at = {0: 2, 1: 2, 2: 5, 3: 5}
+        sums_at = {0: 2, 1: 2, 2: 5, 3: 5, 4: 7, 5: 7}
         for s, lst in multiplies.items():
             for x in lst:
-                if x >= 4:
+                if x >= 2 * WHOLE_UNITS:
                     sums_at[x] = s
         sig = {}
         for x in range(STEPS):
@@ -351,8 +364,10 @@ def tile_vrnncell_pc_kernel(tc, x_t, z_t, a_prev, h_prev, w_ih, w_hh, b_ih, b_hh
 
         bias = None
         both = None
+        keep_warm(WARM[0])
         prepare_activation(0, [x_w, z_w, a_w])
         quantise_activation(0)
+        keep_warm(WARM[1])
         for step in range(total):
             if step % 2 == 0 and step // 2 + LOAD_AHEAD < UNITS:
                 load_unit(step // 2 + LOAD_AHEAD)
@@ -380,10 +395,12 @@ def tile_vrnncell_pc_kernel(tc, x_t, z_t, a_prev, h_prev, w_ih, w_hh, b_ih, b_hh
                 quantise(step, 0, WIDE_SLABS)
                 quantise(step, WIDE_SLABS, STEP_SLABS)
             if step == 0:
+                keep_warm(WARM[2])
                 prepare_activation(1, [h_w[:, :, g * SLAB_WORDS : (g + 1) * SLAB_WORDS] for g in range(PASSES)])
                 quantise_activation(1)
             if step == 1:
                 bias, both = prepare_biases(bias_rows)
+                keep_warm(WARM[3])
             for c, e, x in at(step, "z", 2):
                 if e == 1 and c == CHUNKS - 1:
                     finish_last(c)
@@ -393,5 +410,7 @@ def tile_vrnncell_pc_kernel(tc, x_t, z_t, a_prev, h_prev, w_ih, w_hh, b_ih, b_hh
                 blend_sum(c, e)
             for c, e, x in at(step, "n", 2):
                 candidate_diff(c, e)
+            if step == 4:
+                keep_warm(WARM[4])
             for x in multiplies.get(step, []):
                 multiply_step(x)

@@ -38,7 +38,6 @@ SUM_BANKS = 3
 
 WARM = (6, 3, 2, 2, 2)
 WHOLE_UNITS = 2
-RUN = 1
 
 FLOPS = 2 * 2 * BATCH * K * 3 * HID
 
@@ -241,10 +240,14 @@ def tile_vrnncell_pc_kernel(tc, x_t, z_t, a_prev, h_prev, w_ih, w_hh, b_ih, b_hh
         def column(table, block, chunk, e):
             return table[:, GATE_BLOCK[block] * CHUNKS + chunk, e : e + 1]
 
-        def sigmoid_gate(chunk, e, name, step):
-            gate = gate_tile(chunk, e, name)
+        ALL = slice(0, BATCH)
+
+        def sigmoid_gate(chunk, e, name, step, cols=ALL):
+            if (chunk, e, name) not in gate_tiles:
+                gate_tile(chunk, e, name)
+            gate = gate_tiles[(chunk, e, name)]
             nc.scalar.activation(
-                out=gate[:], in_=sums_of[step][:, 0, :], func=ACT.Sigmoid, bias=column(both, name, chunk, e)
+                out=gate[:, cols], in_=sums_of[step][:, 0, cols], func=ACT.Sigmoid, bias=column(both, name, chunk, e)
             )
 
         def candidate_product(chunk, e, step):
@@ -276,9 +279,11 @@ def tile_vrnncell_pc_kernel(tc, x_t, z_t, a_prev, h_prev, w_ih, w_hh, b_ih, b_hh
                 out=diff[:], in0=h_t[:, g, :, 2 * u + e], in1=gate_tiles[(chunk, e, "n")][:], op=ALU.subtract
             )
 
-        def blend_product(chunk, e):
+        def blend_product(chunk, e, cols=ALL):
             diff = gate_tiles[(chunk, e, "diff")]
-            nc.vector.tensor_tensor(out=diff[:], in0=gate_tiles[(chunk, e, "z")][:], in1=diff[:], op=ALU.mult)
+            nc.vector.tensor_tensor(
+                out=diff[:, cols], in0=gate_tiles[(chunk, e, "z")][:, cols], in1=diff[:, cols], op=ALU.mult
+            )
 
         def blend_sum(chunk, e):
             new = gate_tile(chunk, e, "new")
@@ -286,42 +291,31 @@ def tile_vrnncell_pc_kernel(tc, x_t, z_t, a_prev, h_prev, w_ih, w_hh, b_ih, b_hh
                 out=new[:], in0=gate_tiles[(chunk, e, "diff")][:], in1=gate_tiles[(chunk, e, "n")][:], op=ALU.add
             )
 
-        def transpose_back(chunk):
+        def transpose_back(chunk, h):
             bank = tpsum.tile([P, HALVES, 2, P], F32, tag="bank")
-            for h in range(HALVES):
-                for e in range(2):
-                    nc.tensor.transpose(
-                        bank[:, h, e, :], gate_tiles[(chunk, e, "new")][:, h * P : (h + 1) * P], ident[:]
-                    )
+            for e in range(2):
+                nc.tensor.transpose(
+                    bank[:, 0, e, :], gate_tiles[(chunk, e, "new")][:, h * P : (h + 1) * P], ident[:]
+                )
             return bank
 
-        def finish_last(chunk):
-            banks = []
-            for h in range(HALVES):
-                bank = tpsum.tile([P, HALVES, 2, P], F32, tag="bank")
-                banks.append(bank)
-            for e in range(2):
-                for h in range(HALVES):
-                    nc.tensor.transpose(
-                        banks[h][:, 0, e, :], gate_tiles[(chunk, e, "new")][:, h * P : (h + 1) * P], ident[:]
-                    )
-            for h, engine_copy in enumerate((nc.scalar.copy, nc.vector.tensor_copy)):
-                rows = epool.tile([P, CHUNK], F32, tag="last_rows")
-                engine_copy(
-                    out=rows[:].rearrange("p (q e) -> p q e", e=2), in_=banks[h][:, 0, :, :].rearrange("p e q -> p q e")
-                )
-                nc.sync.dma_start(
-                    out=out.rearrange("(p h) f -> p h f", h=HALVES)[:, h, chunk * CHUNK : (chunk + 1) * CHUNK],
-                    in_=rows[:],
-                )
+        def last_back(banks, e, name, h, start, stop):
+            nc.tensor.matmul(
+                banks[h][:, 0, e, :],
+                lhsT=gate_tiles[(CHUNKS - 1, e, name)][:, h * P : (h + 1) * P],
+                rhs=ident[:],
+                is_transpose=True,
+                start=start,
+                stop=stop,
+            )
 
-        def store_chunk(chunk, bank):
-            rows = epool.tile([P, HALVES, CHUNK], F32, tag="rows")
-            nc.scalar.copy(
-                out=rows[:].rearrange("p h (q e) -> p h q e", e=2), in_=bank[:].rearrange("p h e q -> p h q e")
+        def store_rows(chunk, h, bank, engine_copy):
+            rows = epool.tile([P, CHUNK], F32, tag="rows")
+            engine_copy(
+                out=rows[:].rearrange("p (q e) -> p q e", e=2), in_=bank[:, 0, :, :].rearrange("p e q -> p q e")
             )
             nc.sync.dma_start(
-                out=out.rearrange("(p h) f -> p h f", h=HALVES)[:, :, chunk * CHUNK : (chunk + 1) * CHUNK],
+                out=out.rearrange("(p h) f -> p h f", h=HALVES)[:, h, chunk * CHUNK : (chunk + 1) * CHUNK],
                 in_=rows[:],
             )
 
@@ -342,22 +336,10 @@ def tile_vrnncell_pc_kernel(tc, x_t, z_t, a_prev, h_prev, w_ih, w_hh, b_ih, b_hh
 
         multiplies = {0: [0], 2: [1], 3: [2], 5: [3]}
         for s in range(4, STEPS):
-            at = s + 2
-            if RUN == 2 and at % 2 == 0:
-                at += 1
-            if at >= STEPS + 1:
-                at = STEPS + 1 if s == STEPS - 1 else STEPS
-            multiplies.setdefault(at, []).append(s)
-        sums_at = {0: 2, 1: 2, 2: 5, 3: 5, 4: 7, 5: 7}
-        for s, lst in multiplies.items():
-            for x in lst:
-                if x >= 2 * WHOLE_UNITS:
-                    sums_at[x] = s
-        sig = {}
-        for x in range(STEPS):
-            sig.setdefault(max(sums_at[x] + 1, max(sig, default=0) + 1), []).append(x)
-        sig_step = {x: s for s, lst in sig.items() for x in lst}
-        total = max(sig) + 3
+            multiplies.setdefault(s + 2, []).append(s)
+        sig_step = {0: 3, 1: 4, 2: 6, 3: 6, 4: 8, 5: 8}
+        for x in range(CHUNK_STEPS, STEPS):
+            sig_step[x] = x + 3
 
         def at(step, gate, delay):
             return [half_of(x)[1:] + (x,) for x in range(STEPS) if sig_step[x] + delay == step and half_of(x)[0] == gate]
@@ -368,7 +350,7 @@ def tile_vrnncell_pc_kernel(tc, x_t, z_t, a_prev, h_prev, w_ih, w_hh, b_ih, b_hh
         prepare_activation(0, [x_w, z_w, a_w])
         quantise_activation(0)
         keep_warm(WARM[1])
-        for step in range(total):
+        for step in range(STEPS):
             if step % 2 == 0 and step // 2 + LOAD_AHEAD < UNITS:
                 load_unit(step // 2 + LOAD_AHEAD)
 
@@ -376,21 +358,21 @@ def tile_vrnncell_pc_kernel(tc, x_t, z_t, a_prev, h_prev, w_ih, w_hh, b_ih, b_hh
                 sigmoid_gate(c, e, "r", x)
             for c, e, x in at(step, "z", 0):
                 sigmoid_gate(c, e, "z", x)
-            for c, e, x in at(step, "n", 0):
-                candidate_product(c, e, x)
             for c, e, x in at(step, "n", 1):
                 candidate_tanh(c, e)
             late = step > 3
             if late and 1 <= step <= STEPS:
                 quantise(step - 1, 0, WIDE_SLABS)
             for c, e, x in at(step, "n", 0):
-                candidate_sum(c, e, x)
+                candidate_product(c, e, x)
             for c, e, x in at(step, "z", 1):
                 blend_product(c, e)
             if late and 1 <= step <= STEPS:
                 quantise(step - 1, WIDE_SLABS, STEP_SLABS)
+            for c, e, x in at(step, "n", 0):
+                candidate_sum(c, e, x)
             if step < STEPS:
-                transpose_step(step, vector_banks=(0,) if step % 3 != 1 else ())
+                transpose_step(step, vector_banks=(0,) if step % 2 == 1 else ())
             if step <= 3:
                 quantise(step, 0, WIDE_SLABS)
                 quantise(step, WIDE_SLABS, STEP_SLABS)
@@ -401,11 +383,10 @@ def tile_vrnncell_pc_kernel(tc, x_t, z_t, a_prev, h_prev, w_ih, w_hh, b_ih, b_hh
             if step == 1:
                 bias, both = prepare_biases(bias_rows)
                 keep_warm(WARM[3])
-            for c, e, x in at(step, "z", 2):
-                if e == 1 and c == CHUNKS - 1:
-                    finish_last(c)
-                elif e == 1:
-                    store_chunk(c, transpose_back(c))
+            for h in range(HALVES):
+                for c, e, x in at(step, "z", 2 + h):
+                    if e == 1:
+                        store_rows(c, h, transpose_back(c, h), nc.scalar.copy)
             for c, e, x in at(step, "z", 1):
                 blend_sum(c, e)
             for c, e, x in at(step, "n", 2):
@@ -414,3 +395,35 @@ def tile_vrnncell_pc_kernel(tc, x_t, z_t, a_prev, h_prev, w_ih, w_hh, b_ih, b_hh
                 keep_warm(WARM[4])
             for x in multiplies.get(step, []):
                 multiply_step(x)
+
+        c = CHUNKS - 1
+        n_step, z_step = STEPS - 4, STEPS - 2
+        quantise(STEPS - 1, 0, WIDE_SLABS)
+        quantise(STEPS - 1, WIDE_SLABS, STEP_SLABS)
+        candidate_tanh(c, 0)
+        candidate_product(c, 1, n_step + 1)
+        multiply_step(z_step)
+        candidate_diff(c, 0)
+        candidate_sum(c, 1, n_step + 1)
+        multiply_step(z_step + 1)
+        sigmoid_gate(c, 0, "z", z_step)
+        candidate_tanh(c, 1)
+        blend_product(c, 0)
+        candidate_diff(c, 1)
+        banks = []
+        for h in range(HALVES):
+            bank = tpsum.tile([P, HALVES, 2, P], F32, tag="bank")
+            banks.append(bank)
+        for h in range(HALVES):
+            last_back(banks, 0, "n", h, True, False)
+            last_back(banks, 0, "diff", h, False, True)
+        columns = [slice(h * P, (h + 1) * P) for h in range(HALVES)]
+        for cols in columns:
+            sigmoid_gate(c, 1, "z", z_step + 1, cols)
+        for cols in columns:
+            blend_product(c, 1, cols)
+        for h in range(HALVES):
+            last_back(banks, 1, "n", h, True, False)
+            last_back(banks, 1, "diff", h, False, True)
+        store_rows(c, 0, banks[0], nc.scalar.copy)
+        store_rows(c, 1, banks[1], nc.vector.tensor_copy)

@@ -24,6 +24,8 @@ CHUNKS = HID // CHUNK
 BANK_SLABS = 2
 STEP_SLABS = 2 * PASSES
 STEP_BANKS = STEP_SLABS // BANK_SLABS
+STEP_PASSES = STEP_SLABS
+CLOSE_STEPS = 6
 WIDE_SLABS = 4
 
 GATES = ("r", "n", "z")
@@ -36,7 +38,7 @@ LOAD_AHEAD = 4
 TRANSPOSE_BANKS = 5
 SUM_BANKS = 3
 
-WARM = (6, 3, 2, 2, 2)
+WARM = (6, 3, 2, 2)
 WHOLE_UNITS = 2
 
 FLOPS = 2 * 2 * BATCH * K * 3 * HID
@@ -120,6 +122,8 @@ def tile_vrnncell_pc_kernel(tc, x_t, z_t, a_prev, h_prev, w_ih, w_hh, b_ih, b_hh
                     words[:, b * bank_words : (b + 1) * bank_words],
                     bank,
                 )
+                if b < STEP_BANKS - 1:
+                    multiply_to(passes_after.get(STEP_BANKS * step + b + 1, 0))
             grouped_of[step] = grouped
 
         def quantise(step, first, last):
@@ -214,21 +218,22 @@ def tile_vrnncell_pc_kernel(tc, x_t, z_t, a_prev, h_prev, w_ih, w_hh, b_ih, b_hh
             bank = spsum.tile([P, 2, BATCH], F32, tag="sums")
             sums_of[step] = bank
 
-        def multiply_step(step):
+        passes = []
+        for step in range(STEPS):
             unit, half = divmod(step, 2)
-            apart = GATES[unit % len(GATES)] == "n"
-            if unit < WHOLE_UNITS:
-                if half == 0:
-                    new_sums(2 * unit)
-                    new_sums(2 * unit + 1)
-                for e in range(2):
-                    for g in range(PASSES):
-                        multiply(step, e * PASSES + g, 2 * unit + e, half, g, apart)
-                return
-            new_sums(step)
-            for m in range(2):
+            for j in range(2):
                 for g in range(PASSES):
-                    multiply(step, m * PASSES + g, step, m, g, apart)
+                    m, e = (half, j) if unit < WHOLE_UNITS else (j, half)
+                    passes.append((step, j * PASSES + g, 2 * unit + e, m, g))
+        written = []
+
+        def multiply_to(count):
+            while len(written) < min(count, len(passes)):
+                step, s, out_step, m, g = passes[len(written)]
+                if out_step not in sums_of:
+                    new_sums(out_step)
+                multiply(step, s, out_step, m, g, GATES[step // 2 % len(GATES)] == "n")
+                written.append(step)
 
         gate_tiles = {}
 
@@ -334,10 +339,19 @@ def tile_vrnncell_pc_kernel(tc, x_t, z_t, a_prev, h_prev, w_ih, w_hh, b_ih, b_hh
             load_unit(i)
 
 
-        multiplies = {0: [0], 2: [1], 3: [2], 5: [3]}
-        for s in range(4, STEPS):
-            multiplies.setdefault(s + 2, []).append(s)
-        sig_step = {0: 3, 1: 4, 2: 6, 3: 6, 4: 8, 5: 8}
+        passes_after = {STEP_BANKS: STEP_PASSES}
+        for step in range(2, CLOSE_STEPS):
+            passes_after[STEP_BANKS * (step + 1)] = STEP_PASSES * step
+        banks = STEP_BANKS * CLOSE_STEPS
+        count = STEP_PASSES * (CLOSE_STEPS - 1)
+        for i in range(STEP_BANKS):
+            banks += STEP_BANKS + 1
+            count += STEP_PASSES
+            passes_after[banks] = count
+        for step in range(banks // STEP_BANKS, STEPS):
+            count += STEP_PASSES
+            passes_after[STEP_BANKS * (step + 1)] = count
+        sig_step = {0: 3, 1: 4, 2: 5, 3: 6, 4: 7, 5: 8}
         for x in range(CHUNK_STEPS, STEPS):
             sig_step[x] = x + 3
 
@@ -391,10 +405,7 @@ def tile_vrnncell_pc_kernel(tc, x_t, z_t, a_prev, h_prev, w_ih, w_hh, b_ih, b_hh
                 blend_sum(c, e)
             for c, e, x in at(step, "n", 2):
                 candidate_diff(c, e)
-            if step == 4:
-                keep_warm(WARM[4])
-            for x in multiplies.get(step, []):
-                multiply_step(x)
+            multiply_to(passes_after.get(STEP_BANKS * (step + 1), 0))
 
         c = CHUNKS - 1
         n_step, z_step = STEPS - 4, STEPS - 2
@@ -402,10 +413,10 @@ def tile_vrnncell_pc_kernel(tc, x_t, z_t, a_prev, h_prev, w_ih, w_hh, b_ih, b_hh
         quantise(STEPS - 1, WIDE_SLABS, STEP_SLABS)
         candidate_tanh(c, 0)
         candidate_product(c, 1, n_step + 1)
-        multiply_step(z_step)
+        multiply_to(STEP_PASSES * (STEPS - 1))
         candidate_diff(c, 0)
         candidate_sum(c, 1, n_step + 1)
-        multiply_step(z_step + 1)
+        multiply_to(STEP_PASSES * STEPS)
         sigmoid_gate(c, 0, "z", z_step)
         candidate_tanh(c, 1)
         blend_product(c, 0)

@@ -34,7 +34,7 @@ UNITS = CHUNKS * len(GATES)
 STEPS = 2 * UNITS
 CHUNK_STEPS = 2 * len(GATES)
 
-LOAD_AHEAD = 4
+LOAD_AHEAD = 8
 TRANSPOSE_BANKS = 5
 SUM_BANKS = 3
 
@@ -374,7 +374,7 @@ def tile_vrnncell_pc_kernel(tc, x_t, z_t, a_prev, h_prev, w_ih, w_hh, b_ih, b_hh
                 sigmoid_gate(c, e, "z", x)
             for c, e, x in at(step, "n", 1):
                 candidate_tanh(c, e)
-            late = step > 3
+            late = step > 3 + 1
             if late and 1 <= step <= STEPS:
                 quantise(step - 1, 0, WIDE_SLABS)
             for c, e, x in at(step, "n", 0):

@@ -12,6 +12,7 @@ ACT = mybir.ActivationFunctionType
 ALU = mybir.AluOpType
 
 P = 128
+BLOCK = 32
 BATCH = 256
 HALVES = BATCH // P
 K = 1536
@@ -34,7 +35,7 @@ UNITS = CHUNKS * len(GATES)
 STEPS = 2 * UNITS
 CHUNK_STEPS = 2 * len(GATES)
 
-LOAD_AHEAD = 8
+LOAD_AHEAD = 4
 TRANSPOSE_BANKS = 5
 SUM_BANKS = 3
 
@@ -146,7 +147,9 @@ def tile_vrnncell_pc_kernel(tc, x_t, z_t, a_prev, h_prev, w_ih, w_hh, b_ih, b_hh
         def load_activation(name, src):
             width = src.shape[1]
             t = const.tile([P, HALVES * width], BF16, name="raw_" + name)
-            nc.sync.dma_start(out=t[:], in_=src.rearrange("(p h) k -> p (h k)", h=HALVES))
+            nc.sync.dma_start(
+                out=t[:].rearrange("p (h k) -> p h k", h=HALVES), in_=src.rearrange("(h p) k -> p h k", h=HALVES)
+            )
             return t[:].bitcast(F32).rearrange("p (h w) -> p h w", h=HALVES)
 
         def prepare_activation(m, pass_words):
@@ -238,7 +241,7 @@ def tile_vrnncell_pc_kernel(tc, x_t, z_t, a_prev, h_prev, w_ih, w_hh, b_ih, b_hh
         gate_tiles = {}
 
         def gate_tile(chunk, e, name):
-            t = epool.tile([P, BATCH], F32, tag=name, name="gate_" + name)
+            t = epool.tile([P, BATCH], F32, tag=name, name="gate_" + name, align_bytes=64)
             gate_tiles[(chunk, e, name)] = t
             return t
 
@@ -296,13 +299,24 @@ def tile_vrnncell_pc_kernel(tc, x_t, z_t, a_prev, h_prev, w_ih, w_hh, b_ih, b_hh
                 out=new[:], in0=gate_tiles[(chunk, e, "diff")][:], in1=gate_tiles[(chunk, e, "n")][:], op=ALU.add
             )
 
-        def transpose_back(chunk, h):
-            bank = tpsum.tile([P, HALVES, 2, P], F32, tag="bank")
-            for e in range(2):
-                nc.tensor.transpose(
-                    bank[:, 0, e, :], gate_tiles[(chunk, e, "new")][:, h * P : (h + 1) * P], ident[:]
+        def turn_blocks(chunk, e):
+            if e == 0:
+                turned = epool.tile([P, 2, BATCH], F32, tag="turned", align_bytes=64)
+                gate_tiles[(chunk, "turned")] = turned
+            nc.vector.transpose(gate_tiles[(chunk, "turned")][:, e, :], gate_tiles[(chunk, e, "new")][:])
+
+        def store_turned(chunk):
+            rows = epool.tile([P, 2 * BATCH], F32, tag="turned_rows")
+            nc.scalar.copy(
+                out=rows[:].rearrange("p (n e) -> p n e", e=2),
+                in_=gate_tiles[(chunk, "turned")][:].rearrange("p e n -> p n e"),
+            )
+            for q in range(P // BLOCK):
+                feature = chunk * CHUNK + 2 * BLOCK * q
+                nc.sync.dma_start(
+                    out=out.rearrange("(j a) f -> a j f", a=BLOCK)[:, :, feature : feature + 2 * BLOCK],
+                    in_=rows[BLOCK * q : BLOCK * (q + 1), :].rearrange("a (j f) -> a j f", f=2 * BLOCK),
                 )
-            return bank
 
         def last_back(banks, e, name, h, start, stop):
             nc.tensor.matmul(
@@ -320,7 +334,7 @@ def tile_vrnncell_pc_kernel(tc, x_t, z_t, a_prev, h_prev, w_ih, w_hh, b_ih, b_hh
                 out=rows[:].rearrange("p (q e) -> p q e", e=2), in_=bank[:, 0, :, :].rearrange("p e q -> p q e")
             )
             nc.sync.dma_start(
-                out=out.rearrange("(p h) f -> p h f", h=HALVES)[:, h, chunk * CHUNK : (chunk + 1) * CHUNK],
+                out=out.rearrange("(h p) f -> p h f", h=HALVES)[:, h, chunk * CHUNK : (chunk + 1) * CHUNK],
                 in_=rows[:],
             )
 
@@ -397,10 +411,11 @@ def tile_vrnncell_pc_kernel(tc, x_t, z_t, a_prev, h_prev, w_ih, w_hh, b_ih, b_hh
             if step == 1:
                 bias, both = prepare_biases(bias_rows)
                 keep_warm(WARM[3])
-            for h in range(HALVES):
-                for c, e, x in at(step, "z", 2 + h):
-                    if e == 1:
-                        store_rows(c, h, transpose_back(c, h), nc.scalar.copy)
+            for c, e, x in at(step, "z", 2):
+                turn_blocks(c, e)
+            for c, e, x in at(step, "z", 3):
+                if e == 1:
+                    store_turned(c)
             for c, e, x in at(step, "z", 1):
                 blend_sum(c, e)
             for c, e, x in at(step, "n", 2):

@@ -67,13 +67,11 @@ def tile_vrnncell_pc_kernel(tc, x_t, z_t, a_prev, h_prev, w_ih, w_hh, b_ih, b_hh
         zeros = const.tile([P, 4 * P], BF16)
         nc.vector.memset(zeros[:], 0.0)
 
-        def keep_warm(count):
-            if count == 0:
-                return
-            bank = spsum.tile([P, 2, BATCH], F32, tag="sums")
+        def keep_warm(count, width=4 * P):
+            bank = tpsum.tile([P, 4 * P], F32, tag="bank")
             for i in range(count):
                 nc.tensor.matmul(
-                    bank[:].rearrange("p m b -> p (m b)"), lhsT=zeros[:, 0:P], rhs=zeros[:], start=True, stop=True
+                    bank[:, 0:width], lhsT=zeros[:, 0:P], rhs=zeros[:, 0:width], start=True, stop=True
                 )
 
         def transpose_slabs(slabs):
@@ -123,6 +121,8 @@ def tile_vrnncell_pc_kernel(tc, x_t, z_t, a_prev, h_prev, w_ih, w_hh, b_ih, b_hh
                     words[:, b * bank_words : (b + 1) * bank_words],
                     bank,
                 )
+                if STEP_BANKS * step + b + 1 in close_banks:
+                    keep_warm(1, BATCH)
                 if b < STEP_BANKS - 1:
                     multiply_to(passes_after.get(STEP_BANKS * step + b + 1, 0))
             grouped_of[step] = grouped
@@ -353,6 +353,7 @@ def tile_vrnncell_pc_kernel(tc, x_t, z_t, a_prev, h_prev, w_ih, w_hh, b_ih, b_hh
             load_unit(i)
 
 
+        close_banks = []
         passes_after = {STEP_BANKS: STEP_PASSES}
         for step in range(2, CLOSE_STEPS):
             passes_after[STEP_BANKS * (step + 1)] = STEP_PASSES * step
@@ -362,6 +363,7 @@ def tile_vrnncell_pc_kernel(tc, x_t, z_t, a_prev, h_prev, w_ih, w_hh, b_ih, b_hh
             banks += STEP_BANKS + 1
             count += STEP_PASSES
             passes_after[banks] = count
+            close_banks.append(banks)
         for step in range(banks // STEP_BANKS, STEPS):
             count += STEP_PASSES
             passes_after[STEP_BANKS * (step + 1)] = count

from contextlib import ExitStack

import concourse.mybir as mybir
from concourse.masks import make_identity

F32 = mybir.dt.float32
BF16 = mybir.dt.bfloat16
U32 = mybir.dt.uint32
U8 = mybir.dt.uint8
FP8X4 = mybir.dt.float8_e4m3fn_x4
ACT = mybir.ActivationFunctionType
ALU = mybir.AluOpType

P = 128
BLOCK = 32
BATCH = 256
HALVES = BATCH // P
K = 1536
HID = 1536
K_PASS = 4 * P
PASSES = K // K_PASS
SLAB_WORDS = K_PASS // 2
CHUNK = 2 * P
CHUNKS = HID // CHUNK
BANK_SLABS = 2
STEP_SLABS = 2 * PASSES
STEP_BANKS = STEP_SLABS // BANK_SLABS
STEP_PASSES = STEP_SLABS
CLOSE_STEPS = 6
WIDE_SLABS = 4

GATES = ("r", "n", "z")
GATE_BLOCK = {"r": 0, "z": 1, "n": 2}
UNITS = CHUNKS * len(GATES)
STEPS = 2 * UNITS
CHUNK_STEPS = 2 * len(GATES)

LOAD_AHEAD = 4
TRANSPOSE_BANKS = 5
SUM_BANKS = 3

WARM = (6, 3, 2, 2)
WHOLE_UNITS = 2

FLOPS = 2 * 2 * BATCH * K * 3 * HID


def tile_vrnncell_pc_kernel(tc, x_t, z_t, a_prev, h_prev, w_ih, w_hh, b_ih, b_hh, out):
    nc = tc.nc
    with ExitStack() as ctx:
        const = ctx.enter_context(tc.tile_pool(name="const", bufs=1))
        wpool = ctx.enter_context(tc.tile_pool(name="weights", bufs=2 * (LOAD_AHEAD + 1)))
        gpool = ctx.enter_context(tc.tile_pool(name="grouped", bufs=3))
        qpool = ctx.enter_context(tc.tile_pool(name="quantised", bufs=4))
        epool = ctx.enter_context(tc.tile_pool(name="gates", bufs=4))
        tpsum = ctx.enter_context(tc.psum_pool(name="transposed", bufs=TRANSPOSE_BANKS))
        spsum = ctx.enter_context(tc.psum_pool(name="sums", bufs=SUM_BANKS))
        ctx.enter_context(tc.manual_schedule())

        ident = const.tile([P, P], F32)
        make_identity(nc, ident[:])

        warm = const.tile([P, 1], F32)
        nc.vector.memset(warm[:], 0.0)
        nc.scalar.activation(out=warm[:], in_=warm[:], func=ACT.Sigmoid)

        zeros = const.tile([P, 4 * P], BF16)
        nc.vector.memset(zeros[:], 0.0)

        def keep_warm(count, width=4 * P):
            bank = tpsum.tile([P, 4 * P], F32, tag="bank")
            for i in range(count):
                nc.tensor.matmul(
                    bank[:, 0:width], lhsT=zeros[:, 0:P], rhs=zeros[:, 0:width], start=True, stop=True
                )

        def transpose_slabs(slabs):
            bank = tpsum.tile([P, BANK_SLABS, 2, P], F32, tag="bank")
            for j, words in enumerate(slabs):
                for u in range(2):
                    nc.tensor.transpose(bank[:, j, u, :], words[:, u * P : (u + 1) * P], ident[:])
            return bank

        def copy_grouped(engine_copy, grouped_words, bank):
            engine_copy(
                out=grouped_words.rearrange("p (s r u) -> p s r u", s=BANK_SLABS, u=2),
                in_=bank[:].rearrange("p s u r -> p s r u"),
            )

        weight_words = {}
        grouped_of = {}
        codes_of = {}

        def load_tile(i, m):
            chunk, g = divmod(i, len(GATES))
            row0 = GATE_BLOCK[GATES[g]] * HID + chunk * CHUNK
            wt = wpool.tile([P, 2 * K], BF16, tag="w")
            w = (w_ih, w_hh)[m]
            nc.sync.dma_start(out=wt[:], in_=w[row0 : row0 + CHUNK, :].rearrange("(p e) k -> p (e k)", e=2))
            weight_words[(i, m)] = wt[:].bitcast(F32)

        def load_unit(i):
            load_tile(i, 0)
            load_tile(i, 1)

        def slab_words(step, s):
            unit, half = divmod(step, 2)
            j, g = divmod(s, PASSES)
            m, e = (half, j) if unit < WHOLE_UNITS else (j, half)
            first = (e * PASSES + g) * SLAB_WORDS
            return weight_words[(unit, m)][:, first : first + SLAB_WORDS]

        def transpose_step(step, vector_banks):
            grouped = gpool.tile([P, STEP_SLABS * K_PASS], BF16, tag="grouped", align_bytes=64)
            words = grouped[:].bitcast(F32)
            bank_words = BANK_SLABS * SLAB_WORDS
            for b in range(STEP_BANKS):
                bank = transpose_slabs([slab_words(step, BANK_SLABS * b + j) for j in range(BANK_SLABS)])
                copy_grouped(
                    nc.vector.tensor_copy if b in vector_banks else nc.scalar.copy,
                    words[:, b * bank_words : (b + 1) * bank_words],
                    bank,
                )
                if STEP_BANKS * step + b + 1 in close_banks:
                    keep_warm(1, BATCH)
                if b < STEP_BANKS - 1:
                    multiply_to(passes_after.get(STEP_BANKS * step + b + 1, 0))
            grouped_of[step] = grouped

        def quantise(step, first, last):
            if step not in codes_of:
                codes = qpool.tile([P, STEP_SLABS * P], U32, tag="codes", align_bytes=64)
                scales = qpool.tile([P, STEP_SLABS * P], U8, tag="scales", align_bytes=64)
                codes_of[step] = (codes, scales)
            codes, scales = codes_of[step]
            cols = slice(first * P, last * P)
            nc.vector.quantize_mx(
                out=codes[:, cols].bitcast(FP8X4),
                scales=scales[:, cols],
                in_=grouped_of[step][:, first * K_PASS : last * K_PASS],
            )

        act_codes = []
        act_scales = []
        act_grouped = []

        def load_activation(name, src):
            width = src.shape[1]
            t = const.tile([P, HALVES * width], BF16, name="raw_" + name)
            nc.sync.dma_start(
                out=t[:].rearrange("p (h k) -> p h k", h=HALVES), in_=src.rearrange("(h p) k -> p h k", h=HALVES)
            )
            return t[:].bitcast(F32).rearrange("p (h w) -> p h w", h=HALVES)

        def prepare_activation(m, pass_words):
            grouped = const.tile([P, PASSES * HALVES * K_PASS], BF16, name="act_grouped%d" % m, align_bytes=64)
            words = grouped[:].bitcast(F32)
            for g in range(PASSES):
                bank = transpose_slabs([pass_words[g][:, h, :] for h in range(HALVES)])
                copy_grouped(
                    nc.scalar.copy if g % 2 == 1 else nc.vector.tensor_copy,
                    words[:, g * HALVES * SLAB_WORDS : (g + 1) * HALVES * SLAB_WORDS],
                    bank,
                )
            act_grouped.append(grouped)

        def quantise_activation(m):
            grouped = act_grouped[m]
            codes = const.tile([P, PASSES, BATCH], U32, name="act_codes%d" % m, align_bytes=64)
            scales = const.tile([P, PASSES, BATCH], U8, name="act_scales%d" % m, align_bytes=64)
            for g in range(PASSES):
                nc.vector.quantize_mx(
                    out=codes[:, g, :].bitcast(FP8X4),
                    scales=scales[:, g, :],
                    in_=grouped[:, g * HALVES * K_PASS : (g + 1) * HALVES * K_PASS],
                )
            act_codes.append(codes)
            act_scales.append(scales)

        B_HH_ROW = 32
        BIAS_ROWS = 3 * CHUNKS

        def load_biases():
            bias_rows = const.tile([P, CHUNK], BF16)
            nc.vector.memset(bias_rows[:], 0.0)
            nc.scalar.dma_start(out=bias_rows[0:BIAS_ROWS, :], in_=b_ih.rearrange("(j w) -> j w", w=CHUNK))
            nc.scalar.dma_start(
                out=bias_rows[B_HH_ROW : B_HH_ROW + BIAS_ROWS, :], in_=b_hh.rearrange("(j w) -> j w", w=CHUNK)
            )
            return bias_rows

        def prepare_biases(bias_rows):
            bank = tpsum.tile([P, BANK_SLABS, 2, P], F32, tag="bank")
            nc.tensor.transpose(bank[:, 0, 0, :], bias_rows[:].bitcast(F32), ident[:])
            bias = const.tile([P, P, 2], F32)
            nc.vector.tensor_copy(
                out=bias[:].rearrange("p j e -> p (j e)"), in_=bank[:, 0, 0, :].bitcast(BF16)
            )
            both = const.tile([P, BIAS_ROWS, 2], F32)
            nc.vector.tensor_tensor(
                out=both[:], in0=bias[:, 0:BIAS_ROWS, :], in1=bias[:, B_HH_ROW : B_HH_ROW + BIAS_ROWS, :], op=ALU.add
            )
            return bias, both

        sums_of = {}

        def multiply(step, s, out_step, m, g, apart):
            codes, scales = codes_of[step]
            cols = slice(s * P, (s + 1) * P)
            nc.tensor.matmul_mx(
                out=sums_of[out_step][:, m if apart else 0, :],
                lhsT=codes[:, cols].bitcast(FP8X4),
                lhsT_scale=scales[:, cols],
                rhs=act_codes[m][:, g, :].bitcast(FP8X4),
                rhs_scale=act_scales[m][:, g, :],
                start=(g == 0 and (apart or m == 0)),
                stop=(g == PASSES - 1 and (apart or m == 1)),
            )

        def new_sums(step):
            bank = spsum.tile([P, 2, BATCH], F32, tag="sums")
            sums_of[step] = bank

        passes = []
        for step in range(STEPS):
            unit, half = divmod(step, 2)
            for j in range(2):
                for g in range(PASSES):
                    m, e = (half, j) if unit < WHOLE_UNITS else (j, half)
                    passes.append((step, j * PASSES + g, 2 * unit + e, m, g))
        written = []

        def multiply_to(count):
            while len(written) < min(count, len(passes)):
                step, s, out_step, m, g = passes[len(written)]
                if out_step not in sums_of:
                    new_sums(out_step)
                multiply(step, s, out_step, m, g, GATES[step // 2 % len(GATES)] == "n")
                written.append(step)

        gate_tiles = {}

        def gate_tile(chunk, e, name):
            t = epool.tile([P, BATCH], F32, tag=name, name="gate_" + name, align_bytes=64)
            gate_tiles[(chunk, e, name)] = t
            return t

        def column(table, block, chunk, e):
            return table[:, GATE_BLOCK[block] * CHUNKS + chunk, e : e + 1]

        ALL = slice(0, BATCH)

        def sigmoid_gate(chunk, e, name, step, cols=ALL):
            if (chunk, e, name) not in gate_tiles:
                gate_tile(chunk, e, name)
            gate = gate_tiles[(chunk, e, name)]
            nc.scalar.activation(
                out=gate[:, cols], in_=sums_of[step][:, 0, cols], func=ACT.Sigmoid, bias=column(both, name, chunk, e)
            )

        def candidate_product(chunk, e, step):
            pre = gate_tile(chunk, e, "pre")
            nc.vector.scalar_tensor_tensor(
                out=pre[:],
                in0=sums_of[step][:, 1, :],
                scalar=bias[:, B_HH_ROW + GATE_BLOCK["n"] * CHUNKS + chunk, e : e + 1],
                in1=gate_tiles[(chunk, e, "r")][:],
                op0=ALU.add,
                op1=ALU.mult,
            )

        def candidate_sum(chunk, e, step):
            pre = gate_tiles[(chunk, e, "pre")]
            nc.vector.tensor_tensor(out=pre[:], in0=pre[:], in1=sums_of[step][:, 0, :], op=ALU.add)

        def candidate_tanh(chunk, e):
            n = gate_tile(chunk, e, "n")
            nc.scalar.activation(
                out=n[:], in_=gate_tiles[(chunk, e, "pre")][:], func=ACT.Tanh, bias=column(bias, "n", chunk, e)
            )

        def candidate_diff(chunk, e):
            g, u = divmod(chunk, 2)
            h_t = act_grouped[1][:].rearrange("p (g b t) -> p g b t", g=PASSES, t=4)
            diff = gate_tile(chunk, e, "diff")
            nc.vector.tensor_tensor(
                out=diff[:], in0=h_t[:, g, :, 2 * u + e], in1=gate_tiles[(chunk, e, "n")][:], op=ALU.subtract
            )

        def blend_product(chunk, e, cols=ALL):
            diff = gate_tiles[(chunk, e, "diff")]
            nc.vector.tensor_tensor(
                out=diff[:, cols], in0=gate_tiles[(chunk, e, "z")][:, cols], in1=diff[:, cols], op=ALU.mult
            )

        def blend_sum(chunk, e):
            new = gate_tile(chunk, e, "new")
            nc.vector.tensor_tensor(
                out=new[:], in0=gate_tiles[(chunk, e, "diff")][:], in1=gate_tiles[(chunk, e, "n")][:], op=ALU.add
            )

        def turn_blocks(chunk, e):
            if e == 0:
                turned = epool.tile([P, 2, BATCH], F32, tag="turned", align_bytes=64)
                gate_tiles[(chunk, "turned")] = turned
            nc.vector.transpose(gate_tiles[(chunk, "turned")][:, e, :], gate_tiles[(chunk, e, "new")][:])

        def store_turned(chunk):
            rows = epool.tile([P, 2 * BATCH], F32, tag="turned_rows")
            nc.scalar.copy(
                out=rows[:].rearrange("p (n e) -> p n e", e=2),
                in_=gate_tiles[(chunk, "turned")][:].rearrange("p e n -> p n e"),
            )
            for q in range(P // BLOCK):
                feature = chunk * CHUNK + 2 * BLOCK * q
                nc.sync.dma_start(
                    out=out.rearrange("(j a) f -> a j f", a=BLOCK)[:, :, feature : feature + 2 * BLOCK],
                    in_=rows[BLOCK * q : BLOCK * (q + 1), :].rearrange("a (j f) -> a j f", f=2 * BLOCK),
                )

        def last_back(banks, e, name, h, start, stop):
            nc.tensor.matmul(
                banks[h][:, 0, e, :],
                lhsT=gate_tiles[(CHUNKS - 1, e, name)][:, h * P : (h + 1) * P],
                rhs=ident[:],
                is_transpose=True,
                start=start,
                stop=stop,
            )

        def store_rows(chunk, h, bank, engine_copy):
            rows = epool.tile([P, CHUNK], F32, tag="rows")
            engine_copy(
                out=rows[:].rearrange("p (q e) -> p q e", e=2), in_=bank[:, 0, :, :].rearrange("p e q -> p q e")
            )
            nc.sync.dma_start(
                out=out.rearrange("(h p) f -> p h f", h=HALVES)[:, h, chunk * CHUNK : (chunk + 1) * CHUNK],
                in_=rows[:],
            )

        def half_of(step):
            chunk, rest = divmod(step, CHUNK_STEPS)
            return (GATES[rest // 2] if 0 <= step < STEPS else None), chunk, rest % 2

        x_w = load_activation("x", x_t)
        z_w = load_activation("z", z_t)
        a_w = load_activation("a", a_prev)
        load_tile(0, 0)
        h_w = load_activation("h", h_prev)
        load_tile(0, 1)
        bias_rows = load_biases()
        for i in range(1, LOAD_AHEAD):
            load_unit(i)


        close_banks = []
        passes_after = {STEP_BANKS: STEP_PASSES}
        for step in range(2, CLOSE_STEPS):
            passes_after[STEP_BANKS * (step + 1)] = STEP_PASSES * step
        banks = STEP_BANKS * CLOSE_STEPS
        count = STEP_PASSES * (CLOSE_STEPS - 1)
        for i in range(STEP_BANKS):
            banks += STEP_BANKS + 1
            count += STEP_PASSES
            passes_after[banks] = count
            close_banks.append(banks)
        for step in range(banks // STEP_BANKS, STEPS):
            count += STEP_PASSES
            passes_after[STEP_BANKS * (step + 1)] = count
        sig_step = {0: 3, 1: 4, 2: 5, 3: 6, 4: 7, 5: 8}
        for x in range(CHUNK_STEPS, STEPS):
            sig_step[x] = x + 3

        def at(step, gate, delay):
            return [half_of(x)[1:] + (x,) for x in range(STEPS) if sig_step[x] + delay == step and half_of(x)[0] == gate]

        bias = None
        both = None
        keep_warm(WARM[0])
        prepare_activation(0, [x_w, z_w, a_w])
        quantise_activation(0)
        keep_warm(WARM[1])
        for step in range(STEPS):
            if step % 2 == 0 and step // 2 + LOAD_AHEAD < UNITS:
                load_unit(step // 2 + LOAD_AHEAD)

            for c, e, x in at(step, "r", 0):
                sigmoid_gate(c, e, "r", x)
            for c, e, x in at(step, "z", 0):
                sigmoid_gate(c, e, "z", x)
            for c, e, x in at(step, "n", 1):
                candidate_tanh(c, e)
            late = step > 3 + 1
            if late and 1 <= step <= STEPS:
                quantise(step - 1, 0, WIDE_SLABS)
            for c, e, x in at(step, "n", 0):
                candidate_product(c, e, x)
            for c, e, x in at(step, "z", 1):
                blend_product(c, e)
            if late and 1 <= step <= STEPS:
                quantise(step - 1, WIDE_SLABS, STEP_SLABS)
            for c, e, x in at(step, "n", 0):
                candidate_sum(c, e, x)
            if step < STEPS:
                transpose_step(step, vector_banks=(0,) if step % 2 == 1 else ())
            if step <= 3:
                quantise(step, 0, WIDE_SLABS)
                quantise(step, WIDE_SLABS, STEP_SLABS)
            if step == 0:
                keep_warm(WARM[2])
                prepare_activation(1, [h_w[:, :, g * SLAB_WORDS : (g + 1) * SLAB_WORDS] for g in range(PASSES)])
                quantise_activation(1)
            if step == 1:
                bias, both = prepare_biases(bias_rows)
                keep_warm(WARM[3])
            for c, e, x in at(step, "z", 2):
                turn_blocks(c, e)
            for c, e, x in at(step, "z", 3):
                if e == 1:
                    store_turned(c)
            for c, e, x in at(step, "z", 1):
                blend_sum(c, e)
            for c, e, x in at(step, "n", 2):
                candidate_diff(c, e)
            multiply_to(passes_after.get(STEP_BANKS * (step + 1), 0))

        c = CHUNKS - 1
        n_step, z_step = STEPS - 4, STEPS - 2
        quantise(STEPS - 1, 0, WIDE_SLABS)
        quantise(STEPS - 1, WIDE_SLABS, STEP_SLABS)
        candidate_tanh(c, 0)
        candidate_product(c, 1, n_step + 1)
        multiply_to(STEP_PASSES * (STEPS - 1))
        candidate_diff(c, 0)
        candidate_sum(c, 1, n_step + 1)
        multiply_to(STEP_PASSES * STEPS)
        sigmoid_gate(c, 0, "z", z_step)
        candidate_tanh(c, 1)
        blend_product(c, 0)
        candidate_diff(c, 1)
        banks = []
        for h in range(HALVES):
            bank = tpsum.tile([P, HALVES, 2, P], F32, tag="bank")
            banks.append(bank)
        for h in range(HALVES):
            last_back(banks, 0, "n", h, True, False)
            last_back(banks, 0, "diff", h, False, True)
        columns = [slice(h * P, (h + 1) * P) for h in range(HALVES)]
        for cols in columns:
            sigmoid_gate(c, 1, "z", z_step + 1, cols)
        for cols in columns:
            blend_product(c, 1, cols)
        for h in range(HALVES):
            last_back(banks, 1, "n", h, True, False)
            last_back(banks, 1, "diff", h, False, True)
        store_rows(c, 0, banks[0], nc.scalar.copy)
        store_rows(c, 1, banks[1], nc.vector.tensor_copy)
